import numpy as np
import ml_dtypes


def mxq(x, axis, fmt="e4m3"):
    dtype, down = {"e4m3": (ml_dtypes.float8_e4m3fn, 7), "e5m2": (ml_dtypes.float8_e5m2, 14)}[fmt]
    v = np.moveaxis(np.asarray(x, np.float32).astype(ml_dtypes.bfloat16).astype(np.float64), axis, -1)
    blocks = v.reshape(v.shape[:-1] + (-1, 32))
    amax = np.abs(blocks).max(-1, keepdims=True)
    byte = np.maximum(np.where(amax > 0, np.frexp(amax)[1] - 1 + 127, 0) - down, 1)
    scale = np.exp2(byte - 127.0)
    codes = (blocks / scale).astype(np.float32).astype(dtype).astype(np.float64)
    return np.moveaxis((codes * scale).reshape(v.shape), -1, axis)


WIDE = False


def mx_kscale(k):
    if not WIDE:
        return np.ones(k)
    levels = np.array([20, -20, 10, -10, 0])
    a = np.random.permutation(np.resize(levels, k // 512 * 4)).reshape(k // 512, 4)
    idx = np.arange(k)
    return np.exp2(a[idx // 512, idx % 128 // 32])


BF16 = ml_dtypes.bfloat16


def bf(x):
    return np.asarray(x, np.float32).astype(BF16)


def f64(x):
    return np.asarray(x).astype(np.float64)


S, D = 512, 2048
HALF = D // 2
BASE = 10000.0


def rope_tables():
    freqs = 1.0 / BASE ** (np.arange(HALF) / HALF)
    ang = np.arange(S)[:, None] * freqs[None, :]
    return np.cos(ang), np.sin(ang)


def rope_interleaved(v):
    cos, sin = rope_tables()
    vp = v.reshape(S, HALF, 2)
    vr, vi = vp[..., 0], vp[..., 1]
    rot = np.stack([vr * cos - vi * sin, vr * sin + vi * cos], axis=-1)
    return rot.reshape(S, D)


def rope_interleaved_back(g):
    cos, sin = rope_tables()
    gp = g.reshape(S, HALF, 2)
    gr, gi = gp[..., 0], gp[..., 1]
    rot = np.stack([gr * cos + gi * sin, gi * cos - gr * sin], axis=-1)
    return rot.reshape(S, D)


def setup_inputs():
    s = mx_kscale(S)[:, None]
    x = np.random.standard_normal((S, D)) * s
    w = np.random.standard_normal((D, D)) / np.sqrt(D)
    g = np.random.standard_normal((S, D)) * np.exp2(np.random.randint(-12, 1, (S, 1))) / s
    return {"x": bf(x), "w": bf(w), "grad_out": bf(g)}


def reference(x, w, grad_out):
    gy = rope_interleaved_back(f64(grad_out))
    return mxq(gy, 0, "e5m2").T @ mxq(f64(x), 0, "e4m3")

@@ -1,0 +1,301 @@
+import math
+from contextlib import ExitStack
+
+import concourse.mybir as mybir
+
+F32 = mybir.dt.float32
+BF16 = mybir.dt.bfloat16
+I32 = mybir.dt.int32
+U32 = mybir.dt.uint32
+U8 = mybir.dt.uint8
+E4M3_X4 = mybir.dt.float8_e4m3fn_x4
+E5M2_X4 = mybir.dt.float8_e5m2_x4
+ALU = mybir.AluOpType
+ACT = mybir.ActivationFunctionType
+
+TOKENS = 512
+WIDTH = 2048
+PAIRS = WIDTH // 2
+ROPE_BASE = 10000.0
+TWO_PI = 2.0 * math.pi
+
+P = 128
+PACK = 4
+assert TOKENS == P * PACK
+
+LOAD_COLS = 512
+LOADS = WIDTH // LOAD_COLS
+GROUP_PAIRS = 128
+GROUP_COLS = 2 * GROUP_PAIRS
+GROUPS = PAIRS // GROUP_PAIRS
+N_TILE = 512
+N_TILES = WIDTH // N_TILE
+
+FLOPS = 2 * TOKENS * WIDTH * WIDTH
+BYTES = 2 * (TOKENS * WIDTH * 2) + WIDTH * WIDTH * 4
+
+
+def largest_angle(first_pair):
+    return (TOKENS - 1) * ROPE_BASE ** (-first_pair / PAIRS)
+
+
+WRAPPED_GROUPS = len([g for g in range(GROUPS) if largest_angle(g * GROUP_PAIRS) > math.pi])
+DIRECT_PAIRS = (GROUPS - WRAPPED_GROUPS) * GROUP_PAIRS
+
+
+def regroup(copy, grouped, rows):
+    copy(
+        out=grouped.rearrange("p (c i) t -> p c t i", i=4),
+        in_=rows.rearrange("p t (c i) -> p c t i", i=4),
+    )
+
+
+def tile_ropeattention_pa_kernel(tc, x, w, grad_out, out):
+    nc = tc.nc
+    x_rows = x.rearrange("(p t) c -> p t c", t=PACK)
+    g_rows = grad_out.rearrange("(p t) c -> p t c", t=PACK)
+    out_by_parity = out.rearrange("(i e) c -> e i c", e=2)
+
+    with ExitStack() as stack:
+        keep = stack.enter_context(tc.tile_pool(name="keep", bufs=1))
+        angles = stack.enter_context(tc.tile_pool(name="angles", bufs=3))
+        work = stack.enter_context(tc.tile_pool(name="work", bufs=2))
+        results = stack.enter_context(tc.tile_pool(name="results", bufs=6))
+        banks = stack.enter_context(tc.psum_pool(name="banks", bufs=8))
+        stack.enter_context(tc.manual_schedule())
+
+        x_raw = [keep.tile([P, PACK, LOAD_COLS], BF16, name="x_raw%d" % c) for c in range(LOADS)]
+        g_raw = [keep.tile([P, PACK, LOAD_COLS], BF16, name="g_raw%d" % c) for c in range(LOADS)]
+
+        def load(tiles, rows, c):
+            nc.sync.dma_start(out=tiles[c][:], in_=rows[:, :, c * LOAD_COLS : (c + 1) * LOAD_COLS])
+
+        load(x_raw, x_rows, 0)
+        load(g_raw, g_rows, 0)
+        for c in range(1, LOADS):
+            load(x_raw, x_rows, c)
+        for c in range(1, LOADS):
+            load(g_raw, g_rows, c)
+
+        token_int = keep.tile([P, PACK], I32)
+        nc.gpsimd.iota(out=token_int[:], pattern=[[1, PACK]], base=0, channel_multiplier=PACK)
+        token = keep.tile([P, PACK], F32)
+        nc.vector.tensor_copy(out=token[:], in_=token_int[:])
+        token_radians = keep.tile([P, PACK], F32)
+        nc.vector.tensor_scalar(
+            out=token_radians[:], in0=token[:], scalar1=TWO_PI, scalar2=None, op0=ALU.mult
+        )
+        token_radians_neg = keep.tile([P, PACK], F32)
+        nc.vector.tensor_scalar(
+            out=token_radians_neg[:], in0=token[:], scalar1=-TWO_PI, scalar2=None, op0=ALU.mult
+        )
+
+        one = keep.tile([P, 1], F32)
+        nc.vector.memset(one[:], 1.0)
+        turns = keep.tile([P, PAIRS], F32)
+        nc.vector.tensor_scalar(
+            out=turns[:, 0:1], in0=one[:], scalar1=1.0 / TWO_PI, scalar2=None, op0=ALU.mult
+        )
+        filled = 1
+        while filled < PAIRS:
+            nc.vector.tensor_scalar(
+                out=turns[:, filled : 2 * filled],
+                in0=turns[:, 0:filled],
+                scalar1=ROPE_BASE ** (-filled / PAIRS),
+                scalar2=None,
+                op0=ALU.mult,
+            )
+            filled *= 2
+
+        sin_direct = keep.tile([P, PACK, DIRECT_PAIRS], F32)
+        cos_direct = keep.tile([P, PACK, DIRECT_PAIRS], F32)
+
+        def direct_tables(t):
+            nc.scalar.activation(
+                out=sin_direct[:, t, :],
+                in_=turns[:, PAIRS - DIRECT_PAIRS :],
+                func=ACT.Sin,
+                scale=token_radians[:, t : t + 1],
+            )
+            nc.scalar.activation(
+                out=cos_direct[:, t, :],
+                in_=turns[:, PAIRS - DIRECT_PAIRS :],
+                func=ACT.Sin,
+                scale=token_radians_neg[:, t : t + 1],
+                bias=math.pi / 2.0,
+            )
+
+        tables = {}
+        for g in range(WRAPPED_GROUPS, GROUPS):
+            first = (g - WRAPPED_GROUPS) * GROUP_PAIRS
+            tables[g] = (
+                sin_direct[:, :, first : first + GROUP_PAIRS],
+                cos_direct[:, :, first : first + GROUP_PAIRS],
+            )
+
+        def wrapped_tables(g):
+            pairs = slice(g * GROUP_PAIRS, (g + 1) * GROUP_PAIRS)
+            whole = angles.tile([P, PACK, GROUP_PAIRS], I32)
+            frac = angles.tile([P, PACK, GROUP_PAIRS], F32)
+            for t in range(PACK):
+                nc.vector.tensor_scalar(
+                    out=whole[:, t, :],
+                    in0=turns[:, pairs],
+                    scalar1=token[:, t : t + 1],
+                    scalar2=None,
+                    op0=ALU.mult,
+                )
+            for t in range(PACK):
+                nc.vector.scalar_tensor_tensor(
+                    out=frac[:, t, :],
+                    in0=turns[:, pairs],
+                    scalar=token[:, t : t + 1],
+                    in1=whole[:, t, :],
+                    op0=ALU.mult,
+                    op1=ALU.subtract,
+                )
+            minus_q = angles.tile([P, PACK, GROUP_PAIRS], F32)
+            nc.vector.scalar_tensor_tensor(
+                out=minus_q[:],
+                in0=frac[:],
+                scalar=0.25,
+                in1=frac[:],
+                op0=ALU.is_gt,
+                op1=ALU.subtract,
+            )
+            sin_g = angles.tile([P, PACK, GROUP_PAIRS], F32)
+            nc.scalar.activation(out=sin_g[:], in_=frac[:], func=ACT.Sin, scale=TWO_PI)
+            cos_g = angles.tile([P, PACK, GROUP_PAIRS], F32)
+            nc.scalar.activation(
+                out=cos_g[:], in_=minus_q[:], func=ACT.Sin, scale=-TWO_PI, bias=math.pi / 2.0
+            )
+            tables[g] = (sin_g[:], cos_g[:])
+
+        x_codes = keep.tile([P, WIDTH], U32, align_bytes=64)
+        x_scales = keep.tile([P, WIDTH], U8, align_bytes=64)
+        x_grouped = [
+            keep.tile([P, LOAD_COLS, PACK], BF16, name="x_grouped%d" % c, align_bytes=64)
+            for c in range(LOADS)
+        ]
+
+        def x_regroup(copy, c):
+            regroup(copy, x_grouped[c][:], x_raw[c][:])
+
+        def x_quantise(c):
+            cols = slice(c * LOAD_COLS, (c + 1) * LOAD_COLS)
+            nc.vector.quantize_mx(
+                out=x_codes[:, cols].bitcast(E4M3_X4),
+                scales=x_scales[:, cols],
+                in_=x_grouped[c][:].rearrange("p c t -> p (c t)"),
+            )
+
+        gy_codes = keep.tile([P, GROUPS, 2, GROUP_PAIRS], U32, align_bytes=64)
+        gy_scales = keep.tile([P, GROUPS, 2, GROUP_PAIRS], U8, align_bytes=64)
+        live = {}
+
+        def products(g):
+            sin_g, cos_g = tables[g]
+            first_col = (g * GROUP_COLS) % LOAD_COLS
+            by_parity = g_raw[(g * GROUP_COLS) // LOAD_COLS][
+                :, :, first_col : first_col + GROUP_COLS
+            ].rearrange("p t (i e) -> p e t i", e=2)
+            even_cos = work.tile([P, PACK, GROUP_PAIRS], F32)
+            odd_sin = work.tile([P, PACK, GROUP_PAIRS], F32)
+            odd_cos = work.tile([P, PACK, GROUP_PAIRS], F32)
+            even_sin = work.tile([P, PACK, GROUP_PAIRS], F32)
+            nc.vector.tensor_tensor(out=even_cos[:], in0=by_parity[:, 0], in1=cos_g, op=ALU.mult)
+            nc.vector.tensor_tensor(out=odd_sin[:], in0=by_parity[:, 1], in1=sin_g, op=ALU.mult)
+            nc.vector.tensor_tensor(out=odd_cos[:], in0=by_parity[:, 1], in1=cos_g, op=ALU.mult)
+            nc.vector.tensor_tensor(out=even_sin[:], in0=by_parity[:, 0], in1=sin_g, op=ALU.mult)
+            live["products"] = (even_cos, odd_sin, odd_cos, even_sin)
+
+        def sums(g):
+            even_cos, odd_sin, odd_cos, even_sin = live["products"]
+            gy_even = work.tile([P, PACK, GROUP_PAIRS], BF16)
+            gy_odd = work.tile([P, PACK, GROUP_PAIRS], BF16)
+            nc.vector.tensor_tensor(out=gy_even[:], in0=even_cos[:], in1=odd_sin[:], op=ALU.add)
+            nc.vector.tensor_tensor(out=gy_odd[:], in0=odd_cos[:], in1=even_sin[:], op=ALU.subtract)
+            live["sums"] = (gy_even, gy_odd)
+
+        def regroups(g):
+            even_grouped = work.tile([P, GROUP_PAIRS, PACK], BF16, align_bytes=64)
+            odd_grouped = work.tile([P, GROUP_PAIRS, PACK], BF16, align_bytes=64)
+            regroup(nc.vector.tensor_copy, even_grouped[:], live["sums"][0][:])
+            regroup(nc.vector.tensor_copy, odd_grouped[:], live["sums"][1][:])
+            live["grouped"] = (even_grouped, odd_grouped)
+
+        def quantises(g):
+            for e in range(2):
+                nc.vector.quantize_mx(
+                    out=gy_codes[:, g, e, :].bitcast(E5M2_X4),
+                    scales=gy_scales[:, g, e, :],
+                    in_=live["grouped"][e][:].rearrange("p c t -> p (c t)"),
+                )
+
+        def emptied_by_vector(g, e, n):
+            if g == GROUPS - 1:
+                return n % 2 == 1
+            return g + 2 >= WRAPPED_GROUPS and e == 1 and n == N_TILES - 1
+
+        waiting = []
+
+        def multiply(g, e):
+            result = results.tile([P, WIDTH], F32)
+            for_vector = []
+            for n in range(N_TILES):
+                n_cols = slice(n * N_TILE, (n + 1) * N_TILE)
+                bank = banks.tile([P, N_TILE], F32)
+                nc.tensor.matmul_mx(
+                    out=bank[:],
+                    lhsT=gy_codes[:, g, e, :].bitcast(E5M2_X4),
+                    lhsT_scale=gy_scales[:, g, e, :],
+                    rhs=x_codes[:, n_cols].bitcast(E4M3_X4),
+                    rhs_scale=x_scales[:, n_cols],
+                    start=True,
+                    stop=True,
+                )
+                if emptied_by_vector(g, e, n):
+                    for_vector.append((result[:, n_cols], bank))
+                else:
+                    nc.scalar.copy(out=result[:, n_cols], in_=bank[:])
+            waiting.append((for_vector, out_by_parity[e, g * P : (g + 1) * P, :], result))
+
+        def finish_waiting(only_ready):
+            while waiting and not (only_ready and waiting[0][0]):
+                for_vector, rows, result = waiting.pop(0)
+                for part, bank in for_vector:
+                    nc.vector.tensor_copy(out=part, in_=bank[:])
+                nc.sync.dma_start(out=rows, in_=result[:])
+
+        direct_tables(0)
+        wrapped_tables(0)
+        direct_tables(1)
+        x_regroup(nc.vector.tensor_copy, 0)
+        x_regroup(nc.scalar.copy, 1)
+        x_regroup(nc.scalar.copy, 3)
+        direct_tables(2)
+        direct_tables(3)
+        prepared = 1
+        for g in range(GROUPS):
+            products(g)
+            if g == 0:
+                x_quantise(0)
+                x_regroup(nc.vector.tensor_copy, 2)
+            finish_waiting(only_ready=False)
+            sums(g)
+            if g == 0:
+                x_quantise(1)
+            regroups(g)
+            if g == 0:
+                x_quantise(2)
+            quantises(g)
+            if g == 0:
+                x_quantise(3)
+            multiply(g, 0)
+            finish_waiting(only_ready=True)
+            while prepared < min(g + 3, WRAPPED_GROUPS):
+                wrapped_tables(prepared)
+                prepared += 1
+            multiply(g, 1)
+            finish_waiting(only_ready=True)
+        finish_waiting(only_ready=False)

@@ -191,45 +191,41 @@ def tile_ropeattention_pa_kernel(tc, x, w, grad_out, out):
 
         gy_codes = keep.tile([P, GROUPS, 2, GROUP_PAIRS], U32, align_bytes=64)
         gy_scales = keep.tile([P, GROUPS, 2, GROUP_PAIRS], U8, align_bytes=64)
-        live = {}
-
-        def products(g):
+        def turn_back_and_quantise(g):
             sin_g, cos_g = tables[g]
             first_col = (g * GROUP_COLS) % LOAD_COLS
             by_parity = g_raw[(g * GROUP_COLS) // LOAD_COLS][
                 :, :, first_col : first_col + GROUP_COLS
             ].rearrange("p t (i e) -> p e t i", e=2)
-            even_cos = work.tile([P, PACK, GROUP_PAIRS], F32)
             odd_sin = work.tile([P, PACK, GROUP_PAIRS], F32)
-            odd_cos = work.tile([P, PACK, GROUP_PAIRS], F32)
+            both_cos = work.tile([P, 2, PACK, GROUP_PAIRS], F32)
             even_sin = work.tile([P, PACK, GROUP_PAIRS], F32)
-            nc.vector.tensor_tensor(out=even_cos[:], in0=by_parity[:, 0], in1=cos_g, op=ALU.mult)
             nc.vector.tensor_tensor(out=odd_sin[:], in0=by_parity[:, 1], in1=sin_g, op=ALU.mult)
-            nc.vector.tensor_tensor(out=odd_cos[:], in0=by_parity[:, 1], in1=cos_g, op=ALU.mult)
+            nc.vector.tensor_tensor(
+                out=both_cos[:],
+                in0=by_parity,
+                in1=cos_g.unsqueeze(1).to_broadcast([P, 2, PACK, GROUP_PAIRS]),
+                op=ALU.mult,
+            )
             nc.vector.tensor_tensor(out=even_sin[:], in0=by_parity[:, 0], in1=sin_g, op=ALU.mult)
-            live["products"] = (even_cos, odd_sin, odd_cos, even_sin)
-
-        def sums(g):
-            even_cos, odd_sin, odd_cos, even_sin = live["products"]
-            gy_even = work.tile([P, PACK, GROUP_PAIRS], BF16)
-            gy_odd = work.tile([P, PACK, GROUP_PAIRS], BF16)
-            nc.vector.tensor_tensor(out=gy_even[:], in0=even_cos[:], in1=odd_sin[:], op=ALU.add)
-            nc.vector.tensor_tensor(out=gy_odd[:], in0=odd_cos[:], in1=even_sin[:], op=ALU.subtract)
-            live["sums"] = (gy_even, gy_odd)
-
-        def regroups(g):
-            even_grouped = work.tile([P, GROUP_PAIRS, PACK], BF16, align_bytes=64)
-            odd_grouped = work.tile([P, GROUP_PAIRS, PACK], BF16, align_bytes=64)
-            regroup(nc.vector.tensor_copy, even_grouped[:], live["sums"][0][:])
-            regroup(nc.vector.tensor_copy, odd_grouped[:], live["sums"][1][:])
-            live["grouped"] = (even_grouped, odd_grouped)
-
-        def quantises(g):
+            grouped = work.tile([P, 2, GROUP_PAIRS, PACK], BF16, align_bytes=64)
+            nc.vector.tensor_tensor(
+                out=grouped[:, 0].rearrange("p (c i) t -> p c t i", i=4),
+                in0=both_cos[:, 0].rearrange("p t (c i) -> p c t i", i=4),
+                in1=odd_sin[:].rearrange("p t (c i) -> p c t i", i=4),
+                op=ALU.add,
+            )
+            nc.vector.tensor_tensor(
+                out=grouped[:, 1].rearrange("p (c i) t -> p c t i", i=4),
+                in0=both_cos[:, 1].rearrange("p t (c i) -> p c t i", i=4),
+                in1=even_sin[:].rearrange("p t (c i) -> p c t i", i=4),
+                op=ALU.subtract,
+            )
             for e in range(2):
                 nc.vector.quantize_mx(
                     out=gy_codes[:, g, e, :].bitcast(E5M2_X4),
                     scales=gy_scales[:, g, e, :],
-                    in_=live["grouped"][e][:].rearrange("p c t -> p (c t)"),
+                    in_=grouped[:, e].rearrange("p c t -> p (c t)"),
                 )
 
         def emptied_by_vector(g, e, n):
@@ -240,6 +236,7 @@ def tile_ropeattention_pa_kernel(tc, x, w, grad_out, out):
         waiting = []
 
         def multiply(g, e):
+            rows = out_by_parity[e, g * P : (g + 1) * P, :]
             result = results.tile([P, WIDTH], F32)
             for_vector = []
             for n in range(N_TILES):
@@ -254,11 +251,18 @@ def tile_ropeattention_pa_kernel(tc, x, w, grad_out, out):
                     start=True,
                     stop=True,
                 )
-                if emptied_by_vector(g, e, n):
+                if g == GROUPS - 1:
+                    if emptied_by_vector(g, e, n):
+                        nc.vector.tensor_copy(out=result[:, n_cols], in_=bank[:])
+                    else:
+                        nc.scalar.copy(out=result[:, n_cols], in_=bank[:])
+                    nc.sync.dma_start(out=rows[:, n_cols], in_=result[:, n_cols])
+                elif emptied_by_vector(g, e, n):
                     for_vector.append((result[:, n_cols], bank))
                 else:
                     nc.scalar.copy(out=result[:, n_cols], in_=bank[:])
-            waiting.append((for_vector, out_by_parity[e, g * P : (g + 1) * P, :], result))
+            if g < GROUPS - 1:
+                waiting.append((for_vector, rows, result))
 
         def finish_waiting(only_ready):
             while waiting and not (only_ready and waiting[0][0]):
@@ -273,29 +277,23 @@ def tile_ropeattention_pa_kernel(tc, x, w, grad_out, out):
         x_regroup(nc.vector.tensor_copy, 0)
         x_regroup(nc.scalar.copy, 1)
         x_regroup(nc.scalar.copy, 3)
-        direct_tables(2)
-        direct_tables(3)
         prepared = 1
         for g in range(GROUPS):
-            products(g)
+            turn_back_and_quantise(g)
+            finish_waiting(only_ready=False)
             if g == 0:
                 x_quantise(0)
                 x_regroup(nc.vector.tensor_copy, 2)
-            finish_waiting(only_ready=False)
-            sums(g)
-            if g == 0:
                 x_quantise(1)
-            regroups(g)
-            if g == 0:
                 x_quantise(2)
-            quantises(g)
-            if g == 0:
                 x_quantise(3)
             multiply(g, 0)
+            multiply(g, 1)
             finish_waiting(only_ready=True)
             while prepared < min(g + 3, WRAPPED_GROUPS):
                 wrapped_tables(prepared)
                 prepared += 1
-            multiply(g, 1)
-            finish_waiting(only_ready=True)
+            if g == 0:
+                direct_tables(2)
+                direct_tables(3)
         finish_waiting(only_ready=False)

@@ -2,6 +2,7 @@ import math
 from contextlib import ExitStack
 
 import concourse.mybir as mybir
+from concourse.masks import make_identity
 
 F32 = mybir.dt.float32
 BF16 = mybir.dt.bfloat16
@@ -31,6 +32,9 @@ GROUPS = PAIRS // GROUP_PAIRS
 N_TILE = 512
 N_TILES = WIDTH // N_TILE
 
+VECTOR_BANKS = 1
+AHEAD = 4
+
 FLOPS = 2 * TOKENS * WIDTH * WIDTH
 BYTES = 2 * (TOKENS * WIDTH * 2) + WIDTH * WIDTH * 4
 
@@ -41,6 +45,17 @@ def largest_angle(first_pair):
 
 WRAPPED_GROUPS = len([g for g in range(GROUPS) if largest_angle(g * GROUP_PAIRS) > math.pi])
 DIRECT_PAIRS = (GROUPS - WRAPPED_GROUPS) * GROUP_PAIRS
+
+
+def alternate(first, second):
+    both = []
+    for k in range(max(len(first), len(second))):
+        both.extend(first[k : k + 1])
+        both.extend(second[k : k + 1])
+    return both
+
+
+ORDER = alternate(list(range(WRAPPED_GROUPS)), list(range(WRAPPED_GROUPS, GROUPS)))
 
 
 def regroup(copy, grouped, rows):
@@ -61,7 +76,9 @@ def tile_ropeattention_pa_kernel(tc, x, w, grad_out, out):
         angles = stack.enter_context(tc.tile_pool(name="angles", bufs=3))
         work = stack.enter_context(tc.tile_pool(name="work", bufs=2))
         results = stack.enter_context(tc.tile_pool(name="results", bufs=6))
-        banks = stack.enter_context(tc.psum_pool(name="banks", bufs=8))
+        single = stack.enter_context(tc.tile_pool(name="single", bufs=1))
+        stages = stack.enter_context(tc.psum_pool(name="stages", bufs=2))
+        banks = stack.enter_context(tc.psum_pool(name="banks", bufs=6))
         stack.enter_context(tc.manual_schedule())
 
         x_raw = [keep.tile([P, PACK, LOAD_COLS], BF16, name="x_raw%d" % c) for c in range(LOADS)]
@@ -70,15 +87,21 @@ def tile_ropeattention_pa_kernel(tc, x, w, grad_out, out):
         def load(tiles, rows, c):
             nc.sync.dma_start(out=tiles[c][:], in_=rows[:, :, c * LOAD_COLS : (c + 1) * LOAD_COLS])
 
+        g_loads = []
+        for g in ORDER:
+            if (g * GROUP_COLS) // LOAD_COLS not in g_loads:
+                g_loads.append((g * GROUP_COLS) // LOAD_COLS)
         load(x_raw, x_rows, 0)
-        load(g_raw, g_rows, 0)
+        load(g_raw, g_rows, g_loads[0])
         for c in range(1, LOADS):
             load(x_raw, x_rows, c)
-        for c in range(1, LOADS):
+        for c in g_loads[1:]:
             load(g_raw, g_rows, c)
 
         token_int = keep.tile([P, PACK], I32)
         nc.gpsimd.iota(out=token_int[:], pattern=[[1, PACK]], base=0, channel_multiplier=PACK)
+        identity = keep.tile([P, P], BF16)
+        make_identity(nc, identity[:])
         token = keep.tile([P, PACK], F32)
         nc.vector.tensor_copy(out=token[:], in_=token_int[:])
         token_radians = keep.tile([P, PACK], F32)
@@ -191,78 +214,91 @@ def tile_ropeattention_pa_kernel(tc, x, w, grad_out, out):
 
         gy_codes = keep.tile([P, GROUPS, 2, GROUP_PAIRS], U32, align_bytes=64)
         gy_scales = keep.tile([P, GROUPS, 2, GROUP_PAIRS], U8, align_bytes=64)
-        def turn_back_and_quantise(g):
-            sin_g, cos_g = tables[g]
+        staged = {}
+        terms = {}
+        grouped = {}
+
+        def stage(g):
             first_col = (g * GROUP_COLS) % LOAD_COLS
             by_parity = g_raw[(g * GROUP_COLS) // LOAD_COLS][
                 :, :, first_col : first_col + GROUP_COLS
             ].rearrange("p t (i e) -> p e t i", e=2)
+            staged[g] = stages.tile([P, 2, PACK, GROUP_PAIRS], BF16, name="staged")
+            for e in range(2):
+                nc.tensor.matmul(
+                    out=staged[g][:, e], lhsT=identity[:], rhs=by_parity[:, e], start=True, stop=True
+                )
+
+        def products(g):
+            sin_g, cos_g = tables[g]
             odd_sin = work.tile([P, PACK, GROUP_PAIRS], F32)
             both_cos = work.tile([P, 2, PACK, GROUP_PAIRS], F32)
             even_sin = work.tile([P, PACK, GROUP_PAIRS], F32)
-            nc.vector.tensor_tensor(out=odd_sin[:], in0=by_parity[:, 1], in1=sin_g, op=ALU.mult)
+            nc.vector.tensor_tensor(out=odd_sin[:], in0=staged[g][:, 1], in1=sin_g, op=ALU.mult)
             nc.vector.tensor_tensor(
                 out=both_cos[:],
-                in0=by_parity,
+                in0=staged[g][:],
                 in1=cos_g.unsqueeze(1).to_broadcast([P, 2, PACK, GROUP_PAIRS]),
                 op=ALU.mult,
             )
-            nc.vector.tensor_tensor(out=even_sin[:], in0=by_parity[:, 0], in1=sin_g, op=ALU.mult)
-            grouped = work.tile([P, 2, GROUP_PAIRS, PACK], BF16, align_bytes=64)
-            nc.vector.tensor_tensor(
-                out=grouped[:, 0].rearrange("p (c i) t -> p c t i", i=4),
+            nc.vector.tensor_tensor(out=even_sin[:], in0=staged[g][:, 0], in1=sin_g, op=ALU.mult)
+            terms[g] = (odd_sin, both_cos, even_sin)
+
+        def sums(engine, g):
+            odd_sin, both_cos, even_sin = terms[g]
+            grouped[g] = single.tile([P, 2, GROUP_PAIRS, PACK], BF16, name="grouped", align_bytes=64)
+            engine.tensor_tensor(
+                out=grouped[g][:, 0].rearrange("p (c i) t -> p c t i", i=4),
                 in0=both_cos[:, 0].rearrange("p t (c i) -> p c t i", i=4),
                 in1=odd_sin[:].rearrange("p t (c i) -> p c t i", i=4),
                 op=ALU.add,
             )
-            nc.vector.tensor_tensor(
-                out=grouped[:, 1].rearrange("p (c i) t -> p c t i", i=4),
+            engine.tensor_tensor(
+                out=grouped[g][:, 1].rearrange("p (c i) t -> p c t i", i=4),
                 in0=both_cos[:, 1].rearrange("p t (c i) -> p c t i", i=4),
                 in1=even_sin[:].rearrange("p t (c i) -> p c t i", i=4),
                 op=ALU.subtract,
             )
+
+        def quantise(g):
             for e in range(2):
                 nc.vector.quantize_mx(
                     out=gy_codes[:, g, e, :].bitcast(E5M2_X4),
                     scales=gy_scales[:, g, e, :],
-                    in_=grouped[:, e].rearrange("p c t -> p (c t)"),
+                    in_=grouped[g][:, e].rearrange("p c t -> p (c t)"),
                 )
-
-        def emptied_by_vector(g, e, n):
-            if g == GROUPS - 1:
-                return n % 2 == 1
-            return g + 2 >= WRAPPED_GROUPS and e == 1 and n == N_TILES - 1
 
         waiting = []
 
-        def multiply(g, e):
-            rows = out_by_parity[e, g * P : (g + 1) * P, :]
-            result = results.tile([P, WIDTH], F32)
-            for_vector = []
-            for n in range(N_TILES):
-                n_cols = slice(n * N_TILE, (n + 1) * N_TILE)
-                bank = banks.tile([P, N_TILE], F32)
-                nc.tensor.matmul_mx(
-                    out=bank[:],
-                    lhsT=gy_codes[:, g, e, :].bitcast(E5M2_X4),
-                    lhsT_scale=gy_scales[:, g, e, :],
-                    rhs=x_codes[:, n_cols].bitcast(E4M3_X4),
-                    rhs_scale=x_scales[:, n_cols],
-                    start=True,
-                    stop=True,
-                )
-                if g == GROUPS - 1:
-                    if emptied_by_vector(g, e, n):
-                        nc.vector.tensor_copy(out=result[:, n_cols], in_=bank[:])
+        def multiply(g, last):
+            for e in range(2):
+                rows = out_by_parity[e, g * P : (g + 1) * P, :]
+                result = results.tile([P, WIDTH], F32)
+                for_vector = []
+                for n in range(N_TILES):
+                    n_cols = slice(n * N_TILE, (n + 1) * N_TILE)
+                    bank = banks.tile([P, N_TILE], F32)
+                    nc.tensor.matmul_mx(
+                        out=bank[:],
+                        lhsT=gy_codes[:, g, e, :].bitcast(E5M2_X4),
+                        lhsT_scale=gy_scales[:, g, e, :],
+                        rhs=x_codes[:, n_cols].bitcast(E4M3_X4),
+                        rhs_scale=x_scales[:, n_cols],
+                        start=True,
+                        stop=True,
+                    )
+                    if last:
+                        if n % 2 == 1:
+                            nc.vector.tensor_copy(out=result[:, n_cols], in_=bank[:])
+                        else:
+                            nc.scalar.copy(out=result[:, n_cols], in_=bank[:])
+                        nc.sync.dma_start(out=rows[:, n_cols], in_=result[:, n_cols])
+                    elif e == 1 and n >= N_TILES - VECTOR_BANKS:
+                        for_vector.append((result[:, n_cols], bank))
                     else:
                         nc.scalar.copy(out=result[:, n_cols], in_=bank[:])
-                    nc.sync.dma_start(out=rows[:, n_cols], in_=result[:, n_cols])
-                elif emptied_by_vector(g, e, n):
-                    for_vector.append((result[:, n_cols], bank))
-                else:
-                    nc.scalar.copy(out=result[:, n_cols], in_=bank[:])
-            if g < GROUPS - 1:
-                waiting.append((for_vector, rows, result))
+                if not last:
+                    waiting.append((for_vector, rows, result))
 
         def finish_waiting(only_ready):
             while waiting and not (only_ready and waiting[0][0]):
@@ -271,29 +307,43 @@ def tile_ropeattention_pa_kernel(tc, x, w, grad_out, out):
                     nc.vector.tensor_copy(out=part, in_=bank[:])
                 nc.sync.dma_start(out=rows, in_=result[:])
 
+        def prepare(k):
+            if k < GROUPS and ORDER[k] < WRAPPED_GROUPS:
+                wrapped_tables(ORDER[k])
+
         direct_tables(0)
-        wrapped_tables(0)
+        prepare(0)
         direct_tables(1)
         x_regroup(nc.vector.tensor_copy, 0)
         x_regroup(nc.scalar.copy, 1)
         x_regroup(nc.scalar.copy, 3)
-        prepared = 1
-        for g in range(GROUPS):
-            turn_back_and_quantise(g)
+        direct_tables(2)
+        direct_tables(3)
+        stage(ORDER[0])
+        stage(ORDER[1])
+        products(ORDER[0])
+        stage(ORDER[2])
+        sums(nc.vector, ORDER[0])
+        quantise(ORDER[0])
+        x_quantise(0)
+        x_regroup(nc.vector.tensor_copy, 2)
+        x_quantise(1)
+        x_quantise(2)
+        x_quantise(3)
+        multiply(ORDER[0], last=False)
+        finish_waiting(only_ready=True)
+        for k in range(1, AHEAD):
+            prepare(k)
+        products(ORDER[1])
+        stage(ORDER[3])
+        for k in range(1, GROUPS):
+            sums(nc.gpsimd, ORDER[k])
+            if k + 1 < GROUPS:
+                products(ORDER[k + 1])
+            if k + 3 < GROUPS:
+                stage(ORDER[k + 3])
             finish_waiting(only_ready=False)
-            if g == 0:
-                x_quantise(0)
-                x_regroup(nc.vector.tensor_copy, 2)
-                x_quantise(1)
-                x_quantise(2)
-                x_quantise(3)
-            multiply(g, 0)
-            multiply(g, 1)
+            prepare(k + AHEAD - 1)
+            quantise(ORDER[k])
+            multiply(ORDER[k], last=(k == GROUPS - 1))
             finish_waiting(only_ready=True)
-            while prepared < min(g + 3, WRAPPED_GROUPS):
-                wrapped_tables(prepared)
-                prepared += 1
-            if g == 0:
-                direct_tables(2)
-                direct_tables(3)
-        finish_waiting(only_ready=False)

@@ -2,7 +2,6 @@ import math
 from contextlib import ExitStack
 
 import concourse.mybir as mybir
-from concourse.masks import make_identity
 
 F32 = mybir.dt.float32
 BF16 = mybir.dt.bfloat16
@@ -32,9 +31,6 @@ GROUPS = PAIRS // GROUP_PAIRS
 N_TILE = 512
 N_TILES = WIDTH // N_TILE
 
-VECTOR_BANKS = 1
-AHEAD = 4
-
 FLOPS = 2 * TOKENS * WIDTH * WIDTH
 BYTES = 2 * (TOKENS * WIDTH * 2) + WIDTH * WIDTH * 4
 
@@ -44,18 +40,11 @@ def largest_angle(first_pair):
 
 
 WRAPPED_GROUPS = len([g for g in range(GROUPS) if largest_angle(g * GROUP_PAIRS) > math.pi])
-DIRECT_PAIRS = (GROUPS - WRAPPED_GROUPS) * GROUP_PAIRS
-
-
-def alternate(first, second):
-    both = []
-    for k in range(max(len(first), len(second))):
-        both.extend(first[k : k + 1])
-        both.extend(second[k : k + 1])
-    return both
-
-
-ORDER = alternate(list(range(WRAPPED_GROUPS)), list(range(WRAPPED_GROUPS, GROUPS)))
+WRAPPED_PAIRS = WRAPPED_GROUPS * GROUP_PAIRS
+DIRECT_PAIRS = PAIRS - WRAPPED_PAIRS
+ORDER = list(range(WRAPPED_GROUPS, GROUPS)) + list(range(WRAPPED_GROUPS))
+TABLE_GROUPS = 2
+AHEAD = 2
 
 
 def regroup(copy, grouped, rows):
@@ -73,12 +62,10 @@ def tile_ropeattention_pa_kernel(tc, x, w, grad_out, out):
 
     with ExitStack() as stack:
         keep = stack.enter_context(tc.tile_pool(name="keep", bufs=1))
-        angles = stack.enter_context(tc.tile_pool(name="angles", bufs=3))
+        angles = stack.enter_context(tc.tile_pool(name="angles", bufs=2))
         work = stack.enter_context(tc.tile_pool(name="work", bufs=2))
         results = stack.enter_context(tc.tile_pool(name="results", bufs=6))
-        single = stack.enter_context(tc.tile_pool(name="single", bufs=1))
-        stages = stack.enter_context(tc.psum_pool(name="stages", bufs=2))
-        banks = stack.enter_context(tc.psum_pool(name="banks", bufs=6))
+        banks = stack.enter_context(tc.psum_pool(name="banks", bufs=8))
         stack.enter_context(tc.manual_schedule())
 
         x_raw = [keep.tile([P, PACK, LOAD_COLS], BF16, name="x_raw%d" % c) for c in range(LOADS)]
@@ -100,8 +87,6 @@ def tile_ropeattention_pa_kernel(tc, x, w, grad_out, out):
 
         token_int = keep.tile([P, PACK], I32)
         nc.gpsimd.iota(out=token_int[:], pattern=[[1, PACK]], base=0, channel_multiplier=PACK)
-        identity = keep.tile([P, P], BF16)
-        make_identity(nc, identity[:])
         token = keep.tile([P, PACK], F32)
         nc.vector.tensor_copy(out=token[:], in_=token_int[:])
         token_radians = keep.tile([P, PACK], F32)
@@ -133,33 +118,35 @@ def tile_ropeattention_pa_kernel(tc, x, w, grad_out, out):
         sin_direct = keep.tile([P, PACK, DIRECT_PAIRS], F32)
         cos_direct = keep.tile([P, PACK, DIRECT_PAIRS], F32)
 
-        def direct_tables(t):
-            nc.scalar.activation(
-                out=sin_direct[:, t, :],
-                in_=turns[:, PAIRS - DIRECT_PAIRS :],
-                func=ACT.Sin,
-                scale=token_radians[:, t : t + 1],
-            )
-            nc.scalar.activation(
-                out=cos_direct[:, t, :],
-                in_=turns[:, PAIRS - DIRECT_PAIRS :],
-                func=ACT.Sin,
-                scale=token_radians_neg[:, t : t + 1],
-                bias=math.pi / 2.0,
-            )
-
         tables = {}
-        for g in range(WRAPPED_GROUPS, GROUPS):
-            first = (g - WRAPPED_GROUPS) * GROUP_PAIRS
-            tables[g] = (
-                sin_direct[:, :, first : first + GROUP_PAIRS],
-                cos_direct[:, :, first : first + GROUP_PAIRS],
-            )
 
-        def wrapped_tables(g):
-            pairs = slice(g * GROUP_PAIRS, (g + 1) * GROUP_PAIRS)
-            whole = angles.tile([P, PACK, GROUP_PAIRS], I32)
-            frac = angles.tile([P, PACK, GROUP_PAIRS], F32)
+        def direct_tables(first_group, groups):
+            first = first_group * GROUP_PAIRS
+            pairs = slice(first, first + groups * GROUP_PAIRS)
+            kept = slice(first - WRAPPED_PAIRS, first - WRAPPED_PAIRS + groups * GROUP_PAIRS)
+            for t in range(PACK):
+                nc.scalar.activation(
+                    out=sin_direct[:, t, kept],
+                    in_=turns[:, pairs],
+                    func=ACT.Sin,
+                    scale=token_radians[:, t : t + 1],
+                )
+                nc.scalar.activation(
+                    out=cos_direct[:, t, kept],
+                    in_=turns[:, pairs],
+                    func=ACT.Sin,
+                    scale=token_radians_neg[:, t : t + 1],
+                    bias=math.pi / 2.0,
+                )
+            for g in range(first_group, first_group + groups):
+                of_g = slice(g * GROUP_PAIRS - WRAPPED_PAIRS, (g + 1) * GROUP_PAIRS - WRAPPED_PAIRS)
+                tables[g] = (sin_direct[:, :, of_g], cos_direct[:, :, of_g])
+
+        def wrapped_tables(first_group, groups):
+            width = groups * GROUP_PAIRS
+            pairs = slice(first_group * GROUP_PAIRS, first_group * GROUP_PAIRS + width)
+            whole = angles.tile([P, PACK, width], I32, tag="whole")
+            frac = angles.tile([P, PACK, width], F32, tag="frac")
             for t in range(PACK):
                 nc.vector.tensor_scalar(
                     out=whole[:, t, :],
@@ -177,22 +164,25 @@ def tile_ropeattention_pa_kernel(tc, x, w, grad_out, out):
                     op0=ALU.mult,
                     op1=ALU.subtract,
                 )
-            minus_q = angles.tile([P, PACK, GROUP_PAIRS], F32)
-            nc.vector.scalar_tensor_tensor(
-                out=minus_q[:],
-                in0=frac[:],
-                scalar=0.25,
-                in1=frac[:],
-                op0=ALU.is_gt,
-                op1=ALU.subtract,
-            )
-            sin_g = angles.tile([P, PACK, GROUP_PAIRS], F32)
-            nc.scalar.activation(out=sin_g[:], in_=frac[:], func=ACT.Sin, scale=TWO_PI)
-            cos_g = angles.tile([P, PACK, GROUP_PAIRS], F32)
+            minus_q = angles.tile([P, PACK, width], F32, tag="minus_q")
+            for half in (slice(0, PACK // 2), slice(PACK // 2, PACK)):
+                nc.vector.scalar_tensor_tensor(
+                    out=minus_q[:, half, :],
+                    in0=frac[:, half, :],
+                    scalar=0.25,
+                    in1=frac[:, half, :],
+                    op0=ALU.is_gt,
+                    op1=ALU.subtract,
+                )
+            sin_w = angles.tile([P, PACK, width], F32, tag="sin_w")
+            nc.scalar.activation(out=sin_w[:], in_=frac[:], func=ACT.Sin, scale=TWO_PI)
+            cos_w = angles.tile([P, PACK, width], F32, tag="cos_w")
             nc.scalar.activation(
-                out=cos_g[:], in_=minus_q[:], func=ACT.Sin, scale=-TWO_PI, bias=math.pi / 2.0
+                out=cos_w[:], in_=minus_q[:], func=ACT.Sin, scale=-TWO_PI, bias=math.pi / 2.0
             )
-            tables[g] = (sin_g[:], cos_g[:])
+            for k in range(groups):
+                of_g = slice(k * GROUP_PAIRS, (k + 1) * GROUP_PAIRS)
+                tables[first_group + k] = (sin_w[:, :, of_g], cos_w[:, :, of_g])
 
         x_codes = keep.tile([P, WIDTH], U32, align_bytes=64)
         x_scales = keep.tile([P, WIDTH], U8, align_bytes=64)
@@ -214,136 +204,104 @@ def tile_ropeattention_pa_kernel(tc, x, w, grad_out, out):
 
         gy_codes = keep.tile([P, GROUPS, 2, GROUP_PAIRS], U32, align_bytes=64)
         gy_scales = keep.tile([P, GROUPS, 2, GROUP_PAIRS], U8, align_bytes=64)
-        staged = {}
-        terms = {}
-        grouped = {}
 
-        def stage(g):
+        def multiply(g, e, last):
+            rows = out_by_parity[e, g * P : (g + 1) * P, :]
+            result = results.tile([P, WIDTH], F32)
+            for n in range(N_TILES):
+                n_cols = slice(n * N_TILE, (n + 1) * N_TILE)
+                bank = banks.tile([P, N_TILE], F32)
+                nc.tensor.matmul_mx(
+                    out=bank[:],
+                    lhsT=gy_codes[:, g, e, :].bitcast(E5M2_X4),
+                    lhsT_scale=gy_scales[:, g, e, :],
+                    rhs=x_codes[:, n_cols].bitcast(E4M3_X4),
+                    rhs_scale=x_scales[:, n_cols],
+                    start=True,
+                    stop=True,
+                )
+                if last and n % 2 == 1:
+                    nc.vector.tensor_copy(out=result[:, n_cols], in_=bank[:])
+                else:
+                    nc.scalar.copy(out=result[:, n_cols], in_=bank[:])
+                if last:
+                    nc.sync.dma_start(out=rows[:, n_cols], in_=result[:, n_cols])
+            if not last:
+                nc.sync.dma_start(out=rows, in_=result[:])
+
+        def columns_by_parity(g):
             first_col = (g * GROUP_COLS) % LOAD_COLS
-            by_parity = g_raw[(g * GROUP_COLS) // LOAD_COLS][
+            return g_raw[(g * GROUP_COLS) // LOAD_COLS][
                 :, :, first_col : first_col + GROUP_COLS
             ].rearrange("p t (i e) -> p e t i", e=2)
-            staged[g] = stages.tile([P, 2, PACK, GROUP_PAIRS], BF16, name="staged")
-            for e in range(2):
-                nc.tensor.matmul(
-                    out=staged[g][:, e], lhsT=identity[:], rhs=by_parity[:, e], start=True, stop=True
+
+        def product(g, e, table):
+            term = work.tile([P, PACK, GROUP_PAIRS], F32, tag="term_%d_%d" % (e, table))
+            nc.vector.tensor_tensor(
+                out=term[:], in0=columns_by_parity(g)[:, e], in1=tables[g][table], op=ALU.mult
+            )
+            return term
+
+        SIN, COS = 0, 1
+        started = {}
+
+        def start(g):
+            started[g] = product(g, 1, SIN)
+
+        def finish(g, last, before_multiplying, before_last_quantise):
+            grouped = work.tile([P, 2, GROUP_PAIRS, PACK], BF16, align_bytes=64)
+
+            def combine(e, with_cos, with_sin, op):
+                nc.vector.tensor_tensor(
+                    out=grouped[:, e].rearrange("p (c i) t -> p c t i", i=4),
+                    in0=with_cos[:].rearrange("p t (c i) -> p c t i", i=4),
+                    in1=with_sin[:].rearrange("p t (c i) -> p c t i", i=4),
+                    op=op,
                 )
 
-        def products(g):
-            sin_g, cos_g = tables[g]
-            odd_sin = work.tile([P, PACK, GROUP_PAIRS], F32)
-            both_cos = work.tile([P, 2, PACK, GROUP_PAIRS], F32)
-            even_sin = work.tile([P, PACK, GROUP_PAIRS], F32)
-            nc.vector.tensor_tensor(out=odd_sin[:], in0=staged[g][:, 1], in1=sin_g, op=ALU.mult)
-            nc.vector.tensor_tensor(
-                out=both_cos[:],
-                in0=staged[g][:],
-                in1=cos_g.unsqueeze(1).to_broadcast([P, 2, PACK, GROUP_PAIRS]),
-                op=ALU.mult,
-            )
-            nc.vector.tensor_tensor(out=even_sin[:], in0=staged[g][:, 0], in1=sin_g, op=ALU.mult)
-            terms[g] = (odd_sin, both_cos, even_sin)
-
-        def sums(engine, g):
-            odd_sin, both_cos, even_sin = terms[g]
-            grouped[g] = single.tile([P, 2, GROUP_PAIRS, PACK], BF16, name="grouped", align_bytes=64)
-            engine.tensor_tensor(
-                out=grouped[g][:, 0].rearrange("p (c i) t -> p c t i", i=4),
-                in0=both_cos[:, 0].rearrange("p t (c i) -> p c t i", i=4),
-                in1=odd_sin[:].rearrange("p t (c i) -> p c t i", i=4),
-                op=ALU.add,
-            )
-            engine.tensor_tensor(
-                out=grouped[g][:, 1].rearrange("p (c i) t -> p c t i", i=4),
-                in0=both_cos[:, 1].rearrange("p t (c i) -> p c t i", i=4),
-                in1=even_sin[:].rearrange("p t (c i) -> p c t i", i=4),
-                op=ALU.subtract,
-            )
-
-        def quantise(g):
-            for e in range(2):
+            def quantise(e):
                 nc.vector.quantize_mx(
                     out=gy_codes[:, g, e, :].bitcast(E5M2_X4),
                     scales=gy_scales[:, g, e, :],
-                    in_=grouped[g][:, e].rearrange("p c t -> p (c t)"),
+                    in_=grouped[:, e].rearrange("p c t -> p (c t)"),
                 )
 
-        waiting = []
+            odd_sin = started[g]
+            even_cos = product(g, 0, COS)
+            even_sin = product(g, 0, SIN)
+            combine(0, even_cos, odd_sin, ALU.add)
+            odd_cos = product(g, 1, COS)
+            quantise(0)
+            before_multiplying()
+            multiply(g, 0, last)
+            combine(1, odd_cos, even_sin, ALU.subtract)
+            before_last_quantise()
+            quantise(1)
+            multiply(g, 1, last)
 
-        def multiply(g, last):
-            for e in range(2):
-                rows = out_by_parity[e, g * P : (g + 1) * P, :]
-                result = results.tile([P, WIDTH], F32)
-                for_vector = []
-                for n in range(N_TILES):
-                    n_cols = slice(n * N_TILE, (n + 1) * N_TILE)
-                    bank = banks.tile([P, N_TILE], F32)
-                    nc.tensor.matmul_mx(
-                        out=bank[:],
-                        lhsT=gy_codes[:, g, e, :].bitcast(E5M2_X4),
-                        lhsT_scale=gy_scales[:, g, e, :],
-                        rhs=x_codes[:, n_cols].bitcast(E4M3_X4),
-                        rhs_scale=x_scales[:, n_cols],
-                        start=True,
-                        stop=True,
-                    )
-                    if last:
-                        if n % 2 == 1:
-                            nc.vector.tensor_copy(out=result[:, n_cols], in_=bank[:])
-                        else:
-                            nc.scalar.copy(out=result[:, n_cols], in_=bank[:])
-                        nc.sync.dma_start(out=rows[:, n_cols], in_=result[:, n_cols])
-                    elif e == 1 and n >= N_TILES - VECTOR_BANKS:
-                        for_vector.append((result[:, n_cols], bank))
-                    else:
-                        nc.scalar.copy(out=result[:, n_cols], in_=bank[:])
-                if not last:
-                    waiting.append((for_vector, rows, result))
-
-        def finish_waiting(only_ready):
-            while waiting and not (only_ready and waiting[0][0]):
-                for_vector, rows, result = waiting.pop(0)
-                for part, bank in for_vector:
-                    nc.vector.tensor_copy(out=part, in_=bank[:])
-                nc.sync.dma_start(out=rows, in_=result[:])
-
-        def prepare(k):
-            if k < GROUPS and ORDER[k] < WRAPPED_GROUPS:
-                wrapped_tables(ORDER[k])
-
-        direct_tables(0)
-        prepare(0)
-        direct_tables(1)
+        direct_tables(ORDER[0], 1)
         x_regroup(nc.vector.tensor_copy, 0)
         x_regroup(nc.scalar.copy, 1)
-        x_regroup(nc.scalar.copy, 3)
-        direct_tables(2)
-        direct_tables(3)
-        stage(ORDER[0])
-        stage(ORDER[1])
-        products(ORDER[0])
-        stage(ORDER[2])
-        sums(nc.vector, ORDER[0])
-        quantise(ORDER[0])
-        x_quantise(0)
-        x_regroup(nc.vector.tensor_copy, 2)
-        x_quantise(1)
-        x_quantise(2)
-        x_quantise(3)
-        multiply(ORDER[0], last=False)
-        finish_waiting(only_ready=True)
-        for k in range(1, AHEAD):
-            prepare(k)
-        products(ORDER[1])
-        stage(ORDER[3])
-        for k in range(1, GROUPS):
-            sums(nc.gpsimd, ORDER[k])
-            if k + 1 < GROUPS:
-                products(ORDER[k + 1])
-            if k + 3 < GROUPS:
-                stage(ORDER[k + 3])
-            finish_waiting(only_ready=False)
-            prepare(k + AHEAD - 1)
-            quantise(ORDER[k])
-            multiply(ORDER[k], last=(k == GROUPS - 1))
-            finish_waiting(only_ready=True)
+        x_regroup(nc.scalar.copy, 2)
+        direct_tables(ORDER[1], GROUPS - WRAPPED_GROUPS - 1)
+
+        def rest_of_x():
+            x_regroup(nc.vector.tensor_copy, 3)
+            for c in range(LOADS):
+                x_quantise(c)
+
+        def nothing():
+            return None
+
+        start(ORDER[0])
+        for k in range(GROUPS):
+            ahead = ORDER[k + AHEAD] if k + AHEAD < GROUPS else GROUPS
+            if ahead < WRAPPED_GROUPS and ahead % TABLE_GROUPS == 0:
+                wrapped_tables(ahead, min(TABLE_GROUPS, WRAPPED_GROUPS - ahead))
+            last = k == GROUPS - 1
+            finish(
+                ORDER[k],
+                last,
+                before_multiplying=(rest_of_x if k == 0 else nothing),
+                before_last_quantise=(nothing if last else lambda: start(ORDER[k + 1])),
+            )

@@ -25,26 +25,24 @@ assert TOKENS == P * PACK
 
 LOAD_COLS = 512
 LOADS = WIDTH // LOAD_COLS
-GROUP_PAIRS = 128
-GROUP_COLS = 2 * GROUP_PAIRS
-GROUPS = PAIRS // GROUP_PAIRS
+M_TILE = 128
 N_TILE = 512
 N_TILES = WIDTH // N_TILE
 
 FLOPS = 2 * TOKENS * WIDTH * WIDTH
 BYTES = 2 * (TOKENS * WIDTH * 2) + WIDTH * WIDTH * 4
 
-
-def largest_angle(first_pair):
-    return (TOKENS - 1) * ROPE_BASE ** (-first_pair / PAIRS)
-
-
-WRAPPED_GROUPS = len([g for g in range(GROUPS) if largest_angle(g * GROUP_PAIRS) > math.pi])
-WRAPPED_PAIRS = WRAPPED_GROUPS * GROUP_PAIRS
-DIRECT_PAIRS = PAIRS - WRAPPED_PAIRS
-ORDER = list(range(WRAPPED_GROUPS, GROUPS)) + list(range(WRAPPED_GROUPS))
-TABLE_GROUPS = 2
+WRAPPED_PAIRS = 640
+UNITS = [(640, 128), (768, 128), (896, 128), (0, 128), (128, 128), (256, 128), (384, 128), (512, 128)]
+G_LOADS = [(640, 128), (768, 256), (0, 256), (256, 256), (512, 128)]
+S_REGROUPS = (0, 1)
+STORE_BANKS = 2
+SEEDS = 8
+RADIX = 4
+VB = {(7, 0, 0): (1, 3), (7, 1, 0): (1, 3), (2, 1, 0): (3,), (4, 1, 0): (3,), (6, 1, 0): (3,)}
+DELAY = 5
 AHEAD = 2
+FINE_FROM = 7
 
 
 def regroup(copy, grouped, rows):
@@ -69,239 +67,286 @@ def tile_ropeattention_pa_kernel(tc, x, w, grad_out, out):
         stack.enter_context(tc.manual_schedule())
 
         x_raw = [keep.tile([P, PACK, LOAD_COLS], BF16, name="x_raw%d" % c) for c in range(LOADS)]
-        g_raw = [keep.tile([P, PACK, LOAD_COLS], BF16, name="g_raw%d" % c) for c in range(LOADS)]
+        g_raw = {}
+        for first, pairs in G_LOADS:
+            g_raw[first] = keep.tile([P, PACK, 2 * pairs], BF16, name="g_raw%d" % first)
 
-        def load(tiles, rows, c):
-            nc.sync.dma_start(out=tiles[c][:], in_=rows[:, :, c * LOAD_COLS : (c + 1) * LOAD_COLS])
+        def load_x(c):
+            nc.sync.dma_start(out=x_raw[c][:], in_=x_rows[:, :, c * LOAD_COLS : (c + 1) * LOAD_COLS])
 
-        g_loads = []
-        for g in ORDER:
-            if (g * GROUP_COLS) // LOAD_COLS not in g_loads:
-                g_loads.append((g * GROUP_COLS) // LOAD_COLS)
-        load(x_raw, x_rows, 0)
-        load(g_raw, g_rows, g_loads[0])
-        for c in range(1, LOADS):
-            load(x_raw, x_rows, c)
-        for c in g_loads[1:]:
-            load(g_raw, g_rows, c)
+        def load_g(k):
+            first, pairs = G_LOADS[k]
+            nc.sync.dma_start(out=g_raw[first][:], in_=g_rows[:, :, 2 * first : 2 * (first + pairs)])
+
+        load_g(0)
+        load_x(0)
+        load_x(1)
+        load_x(2)
+        load_x(3)
+        for k in range(1, len(G_LOADS)):
+            load_g(k)
 
         token_int = keep.tile([P, PACK], I32)
         nc.gpsimd.iota(out=token_int[:], pattern=[[1, PACK]], base=0, channel_multiplier=PACK)
-        token = keep.tile([P, PACK], F32)
-        nc.vector.tensor_copy(out=token[:], in_=token_int[:])
-        token_radians = keep.tile([P, PACK], F32)
-        nc.vector.tensor_scalar(
-            out=token_radians[:], in0=token[:], scalar1=TWO_PI, scalar2=None, op0=ALU.mult
-        )
-        token_radians_neg = keep.tile([P, PACK], F32)
-        nc.vector.tensor_scalar(
-            out=token_radians_neg[:], in0=token[:], scalar1=-TWO_PI, scalar2=None, op0=ALU.mult
-        )
-
         one = keep.tile([P, 1], F32)
         nc.vector.memset(one[:], 1.0)
         turns = keep.tile([P, PAIRS], F32)
-        nc.vector.tensor_scalar(
-            out=turns[:, 0:1], in0=one[:], scalar1=1.0 / TWO_PI, scalar2=None, op0=ALU.mult
-        )
-        filled = 1
-        while filled < PAIRS:
+        token = keep.tile([P, PACK], F32)
+        token_radians = keep.tile([P, PACK], F32)
+        token_radians_neg = keep.tile([P, PACK], F32)
+
+        def scaled_copy(first, source_pairs):
             nc.vector.tensor_scalar(
-                out=turns[:, filled : 2 * filled],
-                in0=turns[:, 0:filled],
-                scalar1=ROPE_BASE ** (-filled / PAIRS),
-                scalar2=None,
-                op0=ALU.mult,
+                out=turns[:, first : first + source_pairs], in0=turns[:, 0:source_pairs],
+                scalar1=ROPE_BASE ** (-first / PAIRS), scalar2=None, op0=ALU.mult,
             )
-            filled *= 2
 
-        sin_direct = keep.tile([P, PACK, DIRECT_PAIRS], F32)
-        cos_direct = keep.tile([P, PACK, DIRECT_PAIRS], F32)
+        for i in range(SEEDS):
+            nc.vector.tensor_scalar(out=turns[:, i : i + 1], in0=one[:], scalar1=ROPE_BASE ** (-i / PAIRS) / TWO_PI, scalar2=None, op0=ALU.mult)
+        nc.vector.tensor_copy(out=token[:], in_=token_int[:])
+        filled = SEEDS
+        while filled < M_TILE:
+            for k in range(1, RADIX):
+                scaled_copy(k * filled, filled)
+            filled *= RADIX
+            if filled == SEEDS * RADIX:
+                nc.vector.tensor_scalar(out=token_radians[:], in0=token[:], scalar1=TWO_PI, scalar2=None, op0=ALU.mult)
+                nc.vector.tensor_scalar(out=token_radians_neg[:], in0=token[:], scalar1=-TWO_PI, scalar2=None, op0=ALU.mult)
+        assert filled == M_TILE
+        for first, pairs in UNITS:
+            for block in range(first, first + pairs, M_TILE):
+                if block > 0:
+                    scaled_copy(block, M_TILE)
 
-        tables = {}
+        sin_t = keep.tile([P, PACK, PAIRS], F32)
+        cos_t = keep.tile([P, PACK, PAIRS], F32)
 
-        def direct_tables(first_group, groups):
-            first = first_group * GROUP_PAIRS
-            pairs = slice(first, first + groups * GROUP_PAIRS)
-            kept = slice(first - WRAPPED_PAIRS, first - WRAPPED_PAIRS + groups * GROUP_PAIRS)
+        def direct_tables(first, pairs):
+            cols = slice(first, first + pairs)
             for t in range(PACK):
-                nc.scalar.activation(
-                    out=sin_direct[:, t, kept],
-                    in_=turns[:, pairs],
-                    func=ACT.Sin,
-                    scale=token_radians[:, t : t + 1],
-                )
-                nc.scalar.activation(
-                    out=cos_direct[:, t, kept],
-                    in_=turns[:, pairs],
-                    func=ACT.Sin,
-                    scale=token_radians_neg[:, t : t + 1],
-                    bias=math.pi / 2.0,
-                )
-            for g in range(first_group, first_group + groups):
-                of_g = slice(g * GROUP_PAIRS - WRAPPED_PAIRS, (g + 1) * GROUP_PAIRS - WRAPPED_PAIRS)
-                tables[g] = (sin_direct[:, :, of_g], cos_direct[:, :, of_g])
+                nc.scalar.activation(out=sin_t[:, t, cols], in_=turns[:, cols], func=ACT.Sin, scale=token_radians[:, t : t + 1])
+                nc.scalar.activation(out=cos_t[:, t, cols], in_=turns[:, cols], func=ACT.Sin, scale=token_radians_neg[:, t : t + 1], bias=math.pi / 2.0)
 
-        def wrapped_tables(first_group, groups):
-            width = groups * GROUP_PAIRS
-            pairs = slice(first_group * GROUP_PAIRS, first_group * GROUP_PAIRS + width)
-            whole = angles.tile([P, PACK, width], I32, tag="whole")
-            frac = angles.tile([P, PACK, width], F32, tag="frac")
+        wrapped = {}
+
+        def wrap_a(first, pairs):
+            cols = slice(first, first + pairs)
+            whole = angles.tile([P, PACK, pairs], I32, tag="whole")
+            frac = angles.tile([P, PACK, pairs], F32, tag="frac")
             for t in range(PACK):
-                nc.vector.tensor_scalar(
-                    out=whole[:, t, :],
-                    in0=turns[:, pairs],
-                    scalar1=token[:, t : t + 1],
-                    scalar2=None,
-                    op0=ALU.mult,
-                )
+                nc.vector.tensor_scalar(out=whole[:, t, :], in0=turns[:, cols], scalar1=token[:, t : t + 1], scalar2=None, op0=ALU.mult)
             for t in range(PACK):
-                nc.vector.scalar_tensor_tensor(
-                    out=frac[:, t, :],
-                    in0=turns[:, pairs],
-                    scalar=token[:, t : t + 1],
-                    in1=whole[:, t, :],
-                    op0=ALU.mult,
-                    op1=ALU.subtract,
-                )
-            minus_q = angles.tile([P, PACK, width], F32, tag="minus_q")
+                nc.vector.scalar_tensor_tensor(out=frac[:, t, :], in0=turns[:, cols], scalar=token[:, t : t + 1], in1=whole[:, t, :], op0=ALU.mult, op1=ALU.subtract)
+            wrapped[first] = frac
+
+        def wrap_b(first, pairs):
+            frac = wrapped[first]
+            minus_q = angles.tile([P, PACK, pairs], F32, tag="minus_q")
             for half in (slice(0, PACK // 2), slice(PACK // 2, PACK)):
-                nc.vector.scalar_tensor_tensor(
-                    out=minus_q[:, half, :],
-                    in0=frac[:, half, :],
-                    scalar=0.25,
-                    in1=frac[:, half, :],
-                    op0=ALU.is_gt,
-                    op1=ALU.subtract,
-                )
-            sin_w = angles.tile([P, PACK, width], F32, tag="sin_w")
-            nc.scalar.activation(out=sin_w[:], in_=frac[:], func=ACT.Sin, scale=TWO_PI)
-            cos_w = angles.tile([P, PACK, width], F32, tag="cos_w")
-            nc.scalar.activation(
-                out=cos_w[:], in_=minus_q[:], func=ACT.Sin, scale=-TWO_PI, bias=math.pi / 2.0
-            )
-            for k in range(groups):
-                of_g = slice(k * GROUP_PAIRS, (k + 1) * GROUP_PAIRS)
-                tables[first_group + k] = (sin_w[:, :, of_g], cos_w[:, :, of_g])
+                nc.vector.scalar_tensor_tensor(out=minus_q[:, half, :], in0=frac[:, half, :], scalar=0.25, in1=frac[:, half, :], op0=ALU.is_gt, op1=ALU.subtract)
+            wrapped[first] = (frac, minus_q)
+
+        def wrap_sin(first, pairs):
+            cols = slice(first, first + pairs)
+            frac = wrapped[first][0]
+            nc.scalar.activation(out=sin_t[:, :, cols], in_=frac[:], func=ACT.Sin, scale=TWO_PI)
+
+        def wrap_cos(first, pairs):
+            cols = slice(first, first + pairs)
+            minus_q = wrapped[first][1]
+            nc.scalar.activation(out=cos_t[:, :, cols], in_=minus_q[:], func=ACT.Sin, scale=-TWO_PI, bias=math.pi / 2.0)
 
         x_codes = keep.tile([P, WIDTH], U32, align_bytes=64)
         x_scales = keep.tile([P, WIDTH], U8, align_bytes=64)
-        x_grouped = [
-            keep.tile([P, LOAD_COLS, PACK], BF16, name="x_grouped%d" % c, align_bytes=64)
-            for c in range(LOADS)
-        ]
+        x_grouped = [keep.tile([P, LOAD_COLS, PACK], BF16, name="x_grouped%d" % c, align_bytes=64) for c in range(LOADS)]
 
-        def x_regroup(copy, c):
-            regroup(copy, x_grouped[c][:], x_raw[c][:])
+        def x_regroup(c):
+            regroup(nc.scalar.copy if c in S_REGROUPS else nc.vector.tensor_copy, x_grouped[c][:], x_raw[c][:])
 
         def x_quantise(c):
             cols = slice(c * LOAD_COLS, (c + 1) * LOAD_COLS)
-            nc.vector.quantize_mx(
-                out=x_codes[:, cols].bitcast(E4M3_X4),
-                scales=x_scales[:, cols],
-                in_=x_grouped[c][:].rearrange("p c t -> p (c t)"),
+            nc.vector.quantize_mx(out=x_codes[:, cols].bitcast(E4M3_X4), scales=x_scales[:, cols], in_=x_grouped[c][:].rearrange("p c t -> p (c t)"))
+
+        gy_codes = keep.tile([P, 2, PAIRS], U32, align_bytes=64)
+        gy_scales = keep.tile([P, 2, PAIRS], U8, align_bytes=64)
+
+        open_tiles = {}
+
+        def pass_(m, e, n):
+            n_cols = slice(n * N_TILE, (n + 1) * N_TILE)
+            bank = banks.tile([P, N_TILE], F32)
+            nc.tensor.matmul_mx(
+                out=bank[:], lhsT=gy_codes[:, e, m * M_TILE : (m + 1) * M_TILE].bitcast(E5M2_X4), lhsT_scale=gy_scales[:, e, m * M_TILE : (m + 1) * M_TILE],
+                rhs=x_codes[:, n_cols].bitcast(E4M3_X4), rhs_scale=x_scales[:, n_cols], start=True, stop=True,
             )
+            return bank
 
-        gy_codes = keep.tile([P, GROUPS, 2, GROUP_PAIRS], U32, align_bytes=64)
-        gy_scales = keep.tile([P, GROUPS, 2, GROUP_PAIRS], U8, align_bytes=64)
-
-        def multiply(g, e, last):
-            rows = out_by_parity[e, g * P : (g + 1) * P, :]
-            result = results.tile([P, WIDTH], F32)
-            for n in range(N_TILES):
-                n_cols = slice(n * N_TILE, (n + 1) * N_TILE)
-                bank = banks.tile([P, N_TILE], F32)
-                nc.tensor.matmul_mx(
-                    out=bank[:],
-                    lhsT=gy_codes[:, g, e, :].bitcast(E5M2_X4),
-                    lhsT_scale=gy_scales[:, g, e, :],
-                    rhs=x_codes[:, n_cols].bitcast(E4M3_X4),
-                    rhs_scale=x_scales[:, n_cols],
-                    start=True,
-                    stop=True,
-                )
-                if last and n % 2 == 1:
-                    nc.vector.tensor_copy(out=result[:, n_cols], in_=bank[:])
-                else:
-                    nc.scalar.copy(out=result[:, n_cols], in_=bank[:])
-                if last:
-                    nc.sync.dma_start(out=rows[:, n_cols], in_=result[:, n_cols])
-            if not last:
+        def empty(m, e, n, bank, engine, store_now):
+            n_cols = slice(n * N_TILE, (n + 1) * N_TILE)
+            if (m, e) not in open_tiles:
+                open_tiles[(m, e)] = results.tile([P, WIDTH], F32, name="result")
+            result = open_tiles[(m, e)]
+            if engine == "V":
+                nc.vector.tensor_copy(out=result[:, n_cols], in_=bank[:])
+            else:
+                nc.scalar.copy(out=result[:, n_cols], in_=bank[:])
+            rows = out_by_parity[e, m * M_TILE : (m + 1) * M_TILE, :]
+            if store_now == 1:
+                nc.sync.dma_start(out=rows[:, n_cols], in_=result[:, n_cols])
+            elif store_now == 4:
                 nc.sync.dma_start(out=rows, in_=result[:])
 
-        def columns_by_parity(g):
-            first_col = (g * GROUP_COLS) % LOAD_COLS
-            return g_raw[(g * GROUP_COLS) // LOAD_COLS][
-                :, :, first_col : first_col + GROUP_COLS
-            ].rearrange("p t (i e) -> p e t i", e=2)
+        def store(m, e, n0, n1):
+            cols = slice(n0 * N_TILE, n1 * N_TILE)
+            nc.sync.dma_start(out=out_by_parity[e, m * M_TILE : (m + 1) * M_TILE, cols], in_=open_tiles[(m, e)][:, cols])
 
-        def product(g, e, table):
-            term = work.tile([P, PACK, GROUP_PAIRS], F32, tag="term_%d_%d" % (e, table))
-            nc.vector.tensor_tensor(
-                out=term[:], in0=columns_by_parity(g)[:, e], in1=tables[g][table], op=ALU.mult
-            )
-            return term
+        def multiply(m, e, fine=False, vbanks=()):
+            step = 1 if fine else STORE_BANKS
+            later = []
+            for n in range(N_TILES):
+                bank = pass_(m, e, n)
+                if n in vbanks:
+                    later.append((m, e, n, bank, "V", 0))
+                else:
+                    empty(m, e, n, bank, "S", 0)
+                if (n + 1) % step == 0:
+                    if any(k in vbanks for k in range(n + 1 - step, n + 1)):
+                        later.append((m, e, n + 1 - step, n + 1))
+                    else:
+                        store(m, e, n + 1 - step, n + 1)
+            return later
+
+        def flush(later):
+            for item in later:
+                if len(item) == 4:
+                    store(*item)
+                else:
+                    empty(*item)
+
+        def by_parity(u):
+            first, pairs = UNITS[u]
+            start = max(f for f, n in G_LOADS if f <= first)
+            return g_raw[start][:, :, 2 * (first - start) : 2 * (first - start + pairs)].rearrange("p t (i e) -> p e t i", e=2)
 
         SIN, COS = 0, 1
-        started = {}
+        terms = {}
+        groupeds = {}
 
-        def start(g):
-            started[g] = product(g, 1, SIN)
+        def product(u, e, table):
+            first, pairs = UNITS[u]
+            term = work.tile([P, PACK, pairs], F32, tag="term_%d_%d" % (e, table))
+            nc.vector.tensor_tensor(out=term[:], in0=by_parity(u)[:, e], in1=(sin_t, cos_t)[table][:, :, first : first + pairs], op=ALU.mult)
+            terms[(u, e, table)] = term
 
-        def finish(g, last, before_multiplying, before_last_quantise):
-            grouped = work.tile([P, 2, GROUP_PAIRS, PACK], BF16, align_bytes=64)
-
-            def combine(e, with_cos, with_sin, op):
-                nc.vector.tensor_tensor(
-                    out=grouped[:, e].rearrange("p (c i) t -> p c t i", i=4),
-                    in0=with_cos[:].rearrange("p t (c i) -> p c t i", i=4),
-                    in1=with_sin[:].rearrange("p t (c i) -> p c t i", i=4),
-                    op=op,
-                )
-
-            def quantise(e):
-                nc.vector.quantize_mx(
-                    out=gy_codes[:, g, e, :].bitcast(E5M2_X4),
-                    scales=gy_scales[:, g, e, :],
-                    in_=grouped[:, e].rearrange("p c t -> p (c t)"),
-                )
-
-            odd_sin = started[g]
-            even_cos = product(g, 0, COS)
-            even_sin = product(g, 0, SIN)
-            combine(0, even_cos, odd_sin, ALU.add)
-            odd_cos = product(g, 1, COS)
-            quantise(0)
-            before_multiplying()
-            multiply(g, 0, last)
-            combine(1, odd_cos, even_sin, ALU.subtract)
-            before_last_quantise()
-            quantise(1)
-            multiply(g, 1, last)
-
-        direct_tables(ORDER[0], 1)
-        x_regroup(nc.vector.tensor_copy, 0)
-        x_regroup(nc.scalar.copy, 1)
-        x_regroup(nc.scalar.copy, 2)
-        direct_tables(ORDER[1], GROUPS - WRAPPED_GROUPS - 1)
-
-        def rest_of_x():
-            x_regroup(nc.vector.tensor_copy, 3)
-            for c in range(LOADS):
-                x_quantise(c)
-
-        def nothing():
-            return None
-
-        start(ORDER[0])
-        for k in range(GROUPS):
-            ahead = ORDER[k + AHEAD] if k + AHEAD < GROUPS else GROUPS
-            if ahead < WRAPPED_GROUPS and ahead % TABLE_GROUPS == 0:
-                wrapped_tables(ahead, min(TABLE_GROUPS, WRAPPED_GROUPS - ahead))
-            last = k == GROUPS - 1
-            finish(
-                ORDER[k],
-                last,
-                before_multiplying=(rest_of_x if k == 0 else nothing),
-                before_last_quantise=(nothing if last else lambda: start(ORDER[k + 1])),
+        def combine(u, e):
+            first, pairs = UNITS[u]
+            if u not in groupeds:
+                groupeds[u] = work.tile([P, 2, pairs, PACK], BF16, align_bytes=64, name="grouped")
+            nc.vector.tensor_tensor(
+                out=groupeds[u][:, e].rearrange("p (c i) t -> p c t i", i=4),
+                in0=terms[(u, e, COS)][:].rearrange("p t (c i) -> p c t i", i=4),
+                in1=terms[(u, 1 - e, SIN)][:].rearrange("p t (c i) -> p c t i", i=4),
+                op=(ALU.add if e == 0 else ALU.subtract),
             )
+
+        def quantise(u, e):
+            first, pairs = UNITS[u]
+            nc.vector.quantize_mx(out=gy_codes[:, e, first : first + pairs].bitcast(E5M2_X4), scales=gy_scales[:, e, first : first + pairs], in_=groupeds[u][:, e].rearrange("p c t -> p (c t)"))
+
+        def m_tiles(u):
+            first, pairs = UNITS[u]
+            return range(first // M_TILE, (first + pairs) // M_TILE)
+
+        def tables_v(u):
+            first, pairs = UNITS[u]
+            if first < WRAPPED_PAIRS:
+                wrap_a(first, pairs)
+                wrap_b(first, pairs)
+
+        def tables_s(u):
+            first, pairs = UNITS[u]
+            if first < WRAPPED_PAIRS:
+                wrap_sin(first, pairs)
+                wrap_cos(first, pairs)
+            else:
+                direct_tables(first, pairs)
+
+        m0 = UNITS[0][0] // M_TILE
+        tables_s(0)
+        tables_s(1)
+        FW = min(u for u in range(len(UNITS)) if UNITS[u][0] < WRAPPED_PAIRS)
+        wrap_a(*UNITS[FW])
+        x_regroup(0)
+        product(0, 1, SIN)
+        product(0, 0, COS)
+        product(0, 0, SIN)
+        combine(0, 0)
+        product(0, 1, COS)
+        quantise(0, 0)
+        x_regroup(1)
+        x_quantise(0)
+        b = pass_(m0, 0, 0)
+        combine(0, 1)
+        x_regroup(2)
+        quantise(0, 1)
+        empty(m0, 0, 0, b, "S", 1)
+        b = pass_(m0, 1, 0)
+        empty(m0, 1, 0, b, "S", 1)
+        x_quantise(1)
+        x_regroup(3)
+        x_quantise(2)
+        for n in (1, 2):
+            for e in (0, 1):
+                b = pass_(m0, e, n)
+                empty(m0, e, n, b, "S", 1)
+        wrap_b(*UNITS[FW])
+        x_quantise(3)
+        for e in (0, 1):
+            b = pass_(m0, e, 3)
+            empty(m0, e, 3, b, "S", 1)
+        product(1, 1, SIN)
+        for u in range(2, FW + 1):
+            tables_s(u)
+
+        pending = []
+
+        def tick():
+            for item in pending:
+                item[0] -= 1
+            for item in [i for i in pending if i[0] <= 0]:
+                flush(item[1])
+                pending.remove(item)
+
+        def queue(later):
+            pending.append([DELAY, later])
+
+        for u in range(1, len(UNITS)):
+            last = u == len(UNITS) - 1
+            product(u, 0, COS)
+            tick()
+            product(u, 0, SIN)
+            tick()
+            combine(u, 0)
+            tick()
+            product(u, 1, COS)
+            tick()
+            quantise(u, 0)
+            for m in m_tiles(u):
+                queue(multiply(m, 0, fine=(u >= FINE_FROM), vbanks=VB.get((u, 0, m - m_tiles(u)[0]), ())))
+            combine(u, 1)
+            tick()
+            if not last:
+                product(u + 1, 1, SIN)
+                tick()
+            quantise(u, 1)
+            if FW < u + AHEAD < len(UNITS):
+                first, pairs = UNITS[u + AHEAD]
+                wrap_a(first, pairs)
+                tick()
+                wrap_b(first, pairs)
+                tick()
+                tables_s(u + AHEAD)
+            for m in m_tiles(u):
+                queue(multiply(m, 1, fine=(u >= FINE_FROM), vbanks=VB.get((u, 1, m - m_tiles(u)[0]), ())))
+        for item in pending:
+            flush(item[1])

@@ -32,16 +32,21 @@ N_TILES = WIDTH // N_TILE
 FLOPS = 2 * TOKENS * WIDTH * WIDTH
 BYTES = 2 * (TOKENS * WIDTH * 2) + WIDTH * WIDTH * 4
 
-WRAPPED_PAIRS = 640
-UNITS = [(640, 128), (768, 128), (896, 128), (0, 128), (128, 128), (256, 128), (384, 128), (512, 128)]
-G_LOADS = [(640, 128), (768, 256), (0, 256), (256, 256), (512, 128)]
+WRAPPED_PAIRS = 512
+FOLDED_PAIRS = 640
+SIN_FOLD_TOKEN = math.pi * ROPE_BASE ** (WRAPPED_PAIRS / PAIRS)
+COS_FOLD_TOKEN = 1.5 * math.pi * ROPE_BASE ** (WRAPPED_PAIRS / PAIRS)
+COS_FOLD_PAIRS = 64
+UNITS = [(640, 128), (768, 128), (896, 128), (512, 128), (0, 128), (128, 128), (256, 128), (384, 128)]
+G_LOADS = [(640, 128), (768, 256), (512, 128), (0, 256), (256, 256)]
 S_REGROUPS = (0, 1)
 STORE_BANKS = 2
 SEEDS = 8
 RADIX = 4
-VB = {(7, 0, 0): (1, 3), (7, 1, 0): (1, 3), (2, 1, 0): (3,), (4, 1, 0): (3,), (6, 1, 0): (3,)}
-DELAY = 5
-AHEAD = 2
+VB = {(7, 0, 0): (1, 3), (7, 1, 0): (1, 3), (1, 1, 0): (3,), (2, 1, 0): (3,), (3, 1, 0): (3,), (5, 1, 0): (3,), (6, 1, 0): (3,)}
+DELAY = 4
+TABLES_AT = {(1, 1): (3,), (3, 1): (5,), (4, 1): (6,), (6, 0): (7,)}
+HEAD_WRAP = True
 FINE_FROM = 7
 
 
@@ -92,8 +97,13 @@ def tile_ropeattention_pa_kernel(tc, x, w, grad_out, out):
         nc.vector.memset(one[:], 1.0)
         turns = keep.tile([P, PAIRS], F32)
         token = keep.tile([P, PACK], F32)
-        token_radians = keep.tile([P, PACK], F32)
-        token_radians_neg = keep.tile([P, PACK], F32)
+        radians = keep.tile([P, 2, PACK], F32)
+        token_radians = radians[:, 0, :]
+        token_radians_neg = radians[:, 1, :]
+        beyond = keep.tile([P, 2, PACK], F32)
+        fold_sign = keep.tile([P, 2, PACK], F32)
+        fold_scale = keep.tile([P, 2, PACK], F32)
+        fold_bias = keep.tile([P, 2, PACK], F32)
 
         def scaled_copy(first, source_pairs):
             nc.vector.tensor_scalar(
@@ -110,13 +120,19 @@ def tile_ropeattention_pa_kernel(tc, x, w, grad_out, out):
                 scaled_copy(k * filled, filled)
             filled *= RADIX
             if filled == SEEDS * RADIX:
-                nc.vector.tensor_scalar(out=token_radians[:], in0=token[:], scalar1=TWO_PI, scalar2=None, op0=ALU.mult)
-                nc.vector.tensor_scalar(out=token_radians_neg[:], in0=token[:], scalar1=-TWO_PI, scalar2=None, op0=ALU.mult)
+                nc.vector.tensor_scalar(out=token_radians, in0=token[:], scalar1=TWO_PI, scalar2=None, op0=ALU.mult)
+                nc.vector.tensor_scalar(out=token_radians_neg, in0=token[:], scalar1=-TWO_PI, scalar2=None, op0=ALU.mult)
+                nc.vector.tensor_scalar(out=beyond[:, 0, :], in0=token[:], scalar1=SIN_FOLD_TOKEN, scalar2=None, op0=ALU.is_gt)
+                nc.vector.tensor_scalar(out=beyond[:, 1, :], in0=token[:], scalar1=COS_FOLD_TOKEN, scalar2=None, op0=ALU.is_gt)
         assert filled == M_TILE
+        nc.vector.tensor_scalar(out=fold_sign[:], in0=beyond[:], scalar1=-2.0, scalar2=1.0, op0=ALU.mult, op1=ALU.add)
+        nc.vector.tensor_scalar(out=fold_bias[:, 0, :], in0=beyond[:, 0, :], scalar1=math.pi, scalar2=None, op0=ALU.mult)
+        nc.vector.tensor_scalar(out=fold_bias[:, 1, :], in0=beyond[:, 1, :], scalar1=-TWO_PI, scalar2=math.pi / 2.0, op0=ALU.mult, op1=ALU.add)
         for first, pairs in UNITS:
             for block in range(first, first + pairs, M_TILE):
                 if block > 0:
                     scaled_copy(block, M_TILE)
+        nc.vector.tensor_tensor(out=fold_scale[:], in0=fold_sign[:], in1=radians[:], op=ALU.mult)
 
         sin_t = keep.tile([P, PACK, PAIRS], F32)
         cos_t = keep.tile([P, PACK, PAIRS], F32)
@@ -126,6 +142,15 @@ def tile_ropeattention_pa_kernel(tc, x, w, grad_out, out):
             for t in range(PACK):
                 nc.scalar.activation(out=sin_t[:, t, cols], in_=turns[:, cols], func=ACT.Sin, scale=token_radians[:, t : t + 1])
                 nc.scalar.activation(out=cos_t[:, t, cols], in_=turns[:, cols], func=ACT.Sin, scale=token_radians_neg[:, t : t + 1], bias=math.pi / 2.0)
+
+        def folded_tables(first, pairs):
+            cols = slice(first, first + pairs)
+            low = slice(first, first + COS_FOLD_PAIRS)
+            high = slice(first + COS_FOLD_PAIRS, first + pairs)
+            for t in range(PACK):
+                nc.scalar.activation(out=sin_t[:, t, cols], in_=turns[:, cols], func=ACT.Sin, scale=fold_scale[:, 0, t : t + 1], bias=fold_bias[:, 0, t : t + 1])
+                nc.scalar.activation(out=cos_t[:, t, low], in_=turns[:, low], func=ACT.Sin, scale=fold_scale[:, 1, t : t + 1], bias=fold_bias[:, 1, t : t + 1])
+                nc.scalar.activation(out=cos_t[:, t, high], in_=turns[:, high], func=ACT.Sin, scale=token_radians_neg[:, t : t + 1], bias=math.pi / 2.0)
 
         wrapped = {}
 
@@ -268,6 +293,8 @@ def tile_ropeattention_pa_kernel(tc, x, w, grad_out, out):
             if first < WRAPPED_PAIRS:
                 wrap_sin(first, pairs)
                 wrap_cos(first, pairs)
+            elif first < FOLDED_PAIRS:
+                folded_tables(first, pairs)
             else:
                 direct_tables(first, pairs)
 
@@ -275,7 +302,8 @@ def tile_ropeattention_pa_kernel(tc, x, w, grad_out, out):
         tables_s(0)
         tables_s(1)
         FW = min(u for u in range(len(UNITS)) if UNITS[u][0] < WRAPPED_PAIRS)
-        wrap_a(*UNITS[FW])
+        if HEAD_WRAP:
+            wrap_a(*UNITS[FW])
         x_regroup(0)
         product(0, 1, SIN)
         product(0, 0, COS)
@@ -299,14 +327,16 @@ def tile_ropeattention_pa_kernel(tc, x, w, grad_out, out):
             for e in (0, 1):
                 b = pass_(m0, e, n)
                 empty(m0, e, n, b, "S", 1)
-        wrap_b(*UNITS[FW])
+        if HEAD_WRAP:
+            wrap_b(*UNITS[FW])
         x_quantise(3)
         for e in (0, 1):
             b = pass_(m0, e, 3)
             empty(m0, e, 3, b, "S", 1)
         product(1, 1, SIN)
-        for u in range(2, FW + 1):
-            tables_s(u)
+        tables_s(2)
+        if HEAD_WRAP:
+            tables_s(FW)
 
         pending = []
 
@@ -320,8 +350,19 @@ def tile_ropeattention_pa_kernel(tc, x, w, grad_out, out):
         def queue(later):
             pending.append([DELAY, later])
 
+        def make_tables(u, slot):
+            for j in TABLES_AT.get((u, slot), ()):
+                first, pairs = UNITS[j]
+                if first < WRAPPED_PAIRS:
+                    wrap_a(first, pairs)
+                    tick()
+                    wrap_b(first, pairs)
+                    tick()
+                tables_s(j)
+
         for u in range(1, len(UNITS)):
             last = u == len(UNITS) - 1
+            make_tables(u, 0)
             product(u, 0, COS)
             tick()
             product(u, 0, SIN)
@@ -339,13 +380,7 @@ def tile_ropeattention_pa_kernel(tc, x, w, grad_out, out):
                 product(u + 1, 1, SIN)
                 tick()
             quantise(u, 1)
-            if FW < u + AHEAD < len(UNITS):
-                first, pairs = UNITS[u + AHEAD]
-                wrap_a(first, pairs)
-                tick()
-                wrap_b(first, pairs)
-                tick()
-                tables_s(u + AHEAD)
+            make_tables(u, 1)
             for m in m_tiles(u):
                 queue(multiply(m, 1, fine=(u >= FINE_FROM), vbanks=VB.get((u, 1, m - m_tiles(u)[0]), ())))
         for item in pending:

@@ -43,17 +43,19 @@ S_REGROUPS = (0, 1)
 STORE_BANKS = 2
 SEEDS = 8
 RADIX = 4
-VB = {(7, 0, 0): (1, 3), (7, 1, 0): (1, 3), (1, 1, 0): (3,), (2, 1, 0): (3,), (3, 1, 0): (3,), (5, 1, 0): (3,), (6, 1, 0): (3,)}
+VB = {(7, 0, 0): (1, 3), (7, 1, 0): (1, 3), (1, 1, 0): (3,), (3, 1, 0): (3,), (5, 1, 0): (3,)}
 DELAY = 4
 TABLES_AT = {(1, 1): (3,), (3, 1): (5,), (4, 1): (6,), (6, 0): (7,)}
 HEAD_WRAP = True
 FINE_FROM = 7
+RUN = 8
+STEPS = {(7, 0): 4, (7, 1): 2}
 
 
 def regroup(copy, grouped, rows):
     copy(
-        out=grouped.rearrange("p (c i) t -> p c t i", i=4),
-        in_=rows.rearrange("p t (c i) -> p c t i", i=4),
+        out=grouped.rearrange("p (c i) t -> p c t i", i=RUN),
+        in_=rows.rearrange("p t (c i) -> p c t i", i=RUN),
     )
 
 
@@ -225,8 +227,8 @@ def tile_ropeattention_pa_kernel(tc, x, w, grad_out, out):
             cols = slice(n0 * N_TILE, n1 * N_TILE)
             nc.sync.dma_start(out=out_by_parity[e, m * M_TILE : (m + 1) * M_TILE, cols], in_=open_tiles[(m, e)][:, cols])
 
-        def multiply(m, e, fine=False, vbanks=()):
-            step = 1 if fine else STORE_BANKS
+        def multiply(m, e, fine=2, vbanks=()):
+            step = fine
             later = []
             for n in range(N_TILES):
                 bank = pass_(m, e, n)
@@ -373,7 +375,7 @@ def tile_ropeattention_pa_kernel(tc, x, w, grad_out, out):
             tick()
             quantise(u, 0)
             for m in m_tiles(u):
-                queue(multiply(m, 0, fine=(u >= FINE_FROM), vbanks=VB.get((u, 0, m - m_tiles(u)[0]), ())))
+                queue(multiply(m, 0, fine=STEPS.get((u, 0), STORE_BANKS), vbanks=VB.get((u, 0, m - m_tiles(u)[0]), ())))
             combine(u, 1)
             tick()
             if not last:
@@ -382,6 +384,6 @@ def tile_ropeattention_pa_kernel(tc, x, w, grad_out, out):
             quantise(u, 1)
             make_tables(u, 1)
             for m in m_tiles(u):
-                queue(multiply(m, 1, fine=(u >= FINE_FROM), vbanks=VB.get((u, 1, m - m_tiles(u)[0]), ())))
+                queue(multiply(m, 1, fine=STEPS.get((u, 1), STORE_BANKS), vbanks=VB.get((u, 1, m - m_tiles(u)[0]), ())))
         for item in pending:
             flush(item[1])

@@ -314,11 +314,13 @@ def tile_ropeattention_pa_kernel(tc, x, w, grad_out, out):
         product(0, 1, COS)
         quantise(0, 0)
         x_regroup(1)
+        tables_s(2)
+        combine(0, 1)
+        wrap_b(*UNITS[FW])
         x_quantise(0)
         b = pass_(m0, 0, 0)
-        combine(0, 1)
-        x_regroup(2)
         quantise(0, 1)
+        x_regroup(2)
         empty(m0, 0, 0, b, "S", 1)
         b = pass_(m0, 1, 0)
         empty(m0, 1, 0, b, "S", 1)
@@ -329,14 +331,11 @@ def tile_ropeattention_pa_kernel(tc, x, w, grad_out, out):
             for e in (0, 1):
                 b = pass_(m0, e, n)
                 empty(m0, e, n, b, "S", 1)
-        if HEAD_WRAP:
-            wrap_b(*UNITS[FW])
         x_quantise(3)
         for e in (0, 1):
             b = pass_(m0, e, 3)
             empty(m0, e, 3, b, "S", 1)
         product(1, 1, SIN)
-        tables_s(2)
         if HEAD_WRAP:
             tables_s(FW)
 

@@ -2,6 +2,7 @@ import math
 from contextlib import ExitStack
 
 import concourse.mybir as mybir
+from concourse.masks import make_identity
 
 F32 = mybir.dt.float32
 BF16 = mybir.dt.bfloat16
@@ -45,7 +46,12 @@ SEEDS = 8
 RADIX = 4
 VB = {(7, 0, 0): (1, 3), (7, 1, 0): (1, 3), (1, 1, 0): (3,), (3, 1, 0): (3,), (5, 1, 0): (3,)}
 DELAY = 4
-TABLES_AT = {(1, 1): (3,), (3, 1): (5,), (4, 1): (6,), (6, 0): (7,)}
+TABLES_AT = {(1, 0): (3,), (3, 1): (5,), (4, 1): (6,), (5, 1): (7,)}
+WRAP_A = {(3, 0): (5,), (4, 0): (6,), (5, 0): (7,)}
+WRAP_B = {(3, 1): (5,), (4, 1): (6,), (5, 1): (7,)}
+VG = {(2,0):(0,),(2,1):(0,),(3,0):(0,),(3,1):(0,),(4,0):(0,),(4,1):(0,),(5,0):(0,),(5,1):(0,),(6,0):(0,),(6,1):(0,),(7,0):(1,3),(7,1):(1,3)}
+STAGED = range(2, 7)
+GUNITS = (2, 3, 4, 5, 6)
 HEAD_WRAP = True
 FINE_FROM = 7
 RUN = 8
@@ -70,7 +76,9 @@ def tile_ropeattention_pa_kernel(tc, x, w, grad_out, out):
         angles = stack.enter_context(tc.tile_pool(name="angles", bufs=2))
         work = stack.enter_context(tc.tile_pool(name="work", bufs=2))
         results = stack.enter_context(tc.tile_pool(name="results", bufs=6))
-        banks = stack.enter_context(tc.psum_pool(name="banks", bufs=8))
+        banks = stack.enter_context(tc.psum_pool(name="banks", bufs=6))
+        staging = stack.enter_context(tc.psum_pool(name="staging", bufs=2))
+        sums = stack.enter_context(tc.tile_pool(name="sums", bufs=1))
         stack.enter_context(tc.manual_schedule())
 
         x_raw = [keep.tile([P, PACK, LOAD_COLS], BF16, name="x_raw%d" % c) for c in range(LOADS)]
@@ -95,6 +103,8 @@ def tile_ropeattention_pa_kernel(tc, x, w, grad_out, out):
 
         token_int = keep.tile([P, PACK], I32)
         nc.gpsimd.iota(out=token_int[:], pattern=[[1, PACK]], base=0, channel_multiplier=PACK)
+        identity = keep.tile([P, P], BF16)
+        make_identity(nc, identity[:])
         one = keep.tile([P, 1], F32)
         nc.vector.memset(one[:], 1.0)
         turns = keep.tile([P, PAIRS], F32)
@@ -259,10 +269,22 @@ def tile_ropeattention_pa_kernel(tc, x, w, grad_out, out):
         terms = {}
         groupeds = {}
 
+        staged = {}
+
+        def stage(u):
+            first, pairs = UNITS[u]
+            start = max(f for f, n in G_LOADS if f <= first)
+            cols = slice(2 * (first - start), 2 * (first - start + pairs))
+            bank = staging.tile([P, PACK, 2 * pairs], BF16, name="staged")
+            for half in (slice(0, PACK // 2), slice(PACK // 2, PACK)):
+                nc.tensor.matmul(bank[:, half, :], lhsT=identity[:], rhs=g_raw[start][:, half, cols], start=True, stop=True)
+            staged[u] = bank[:].rearrange("p t (i e) -> p e t i", e=2)
+
         def product(u, e, table):
             first, pairs = UNITS[u]
             term = work.tile([P, PACK, pairs], F32, tag="term_%d_%d" % (e, table))
-            nc.vector.tensor_tensor(out=term[:], in0=by_parity(u)[:, e], in1=(sin_t, cos_t)[table][:, :, first : first + pairs], op=ALU.mult)
+            g_pairs = staged[u] if u in staged else by_parity(u)
+            nc.vector.tensor_tensor(out=term[:], in0=g_pairs[:, e], in1=(sin_t, cos_t)[table][:, :, first : first + pairs], op=ALU.mult)
             terms[(u, e, table)] = term
 
         def combine(u, e):
@@ -275,6 +297,23 @@ def tile_ropeattention_pa_kernel(tc, x, w, grad_out, out):
                 in1=terms[(u, 1 - e, SIN)][:].rearrange("p t (c i) -> p c t i", i=4),
                 op=(ALU.add if e == 0 else ALU.subtract),
             )
+
+        def combine_g(u, e):
+            first, pairs = UNITS[u]
+            grouped = sums.tile([P, pairs, PACK], BF16, align_bytes=64, name="summed")
+            nc.gpsimd.tensor_tensor(
+                out=grouped[:].rearrange("p (c i) t -> p c t i", i=4),
+                in0=terms[(u, e, COS)][:].rearrange("p t (c i) -> p c t i", i=4),
+                in1=terms[(u, 1 - e, SIN)][:].rearrange("p t (c i) -> p c t i", i=4),
+                op=(ALU.add if e == 0 else ALU.subtract),
+            )
+            summed[(u, e)] = grouped
+
+        summed = {}
+
+        def quantise_g(u, e):
+            first, pairs = UNITS[u]
+            nc.vector.quantize_mx(out=gy_codes[:, e, first : first + pairs].bitcast(E5M2_X4), scales=gy_scales[:, e, first : first + pairs], in_=summed[(u, e)][:].rearrange("p c t -> p (c t)"))
 
         def quantise(u, e):
             first, pairs = UNITS[u]
@@ -331,6 +370,7 @@ def tile_ropeattention_pa_kernel(tc, x, w, grad_out, out):
             for e in (0, 1):
                 b = pass_(m0, e, n)
                 empty(m0, e, n, b, "S", 1)
+        stage(2)
         x_quantise(3)
         for e in (0, 1):
             b = pass_(m0, e, 3)
@@ -339,50 +379,63 @@ def tile_ropeattention_pa_kernel(tc, x, w, grad_out, out):
         if HEAD_WRAP:
             tables_s(FW)
 
-        pending = []
-
-        def tick():
-            for item in pending:
-                item[0] -= 1
-            for item in [i for i in pending if i[0] <= 0]:
-                flush(item[1])
-                pending.remove(item)
-
-        def queue(later):
-            pending.append([DELAY, later])
-
-        def make_tables(u, slot):
-            for j in TABLES_AT.get((u, slot), ()):
-                first, pairs = UNITS[j]
-                if first < WRAPPED_PAIRS:
-                    wrap_a(first, pairs)
-                    tick()
-                    wrap_b(first, pairs)
-                    tick()
+        def make_tables(where):
+            for j in WRAP_A.get(where, ()):
+                wrap_a(*UNITS[j])
+            for j in WRAP_B.get(where, ()):
+                wrap_b(*UNITS[j])
+            for j in TABLES_AT.get(where, ()):
                 tables_s(j)
 
+        def mult(u, e):
+            return multiply(UNITS[u][0] // M_TILE, e, fine=STEPS.get((u, e), STORE_BANKS), vbanks=VG.get((u, e), ()))
+
+        def opt_stage(u):
+            if u in STAGED:
+                stage(u)
+
+        later = []
+        waiting = None
         for u in range(1, len(UNITS)):
             last = u == len(UNITS) - 1
-            make_tables(u, 0)
-            product(u, 0, COS)
-            tick()
-            product(u, 0, SIN)
-            tick()
-            combine(u, 0)
-            tick()
-            product(u, 1, COS)
-            tick()
-            quantise(u, 0)
-            for m in m_tiles(u):
-                queue(multiply(m, 0, fine=STEPS.get((u, 0), STORE_BANKS), vbanks=VB.get((u, 0, m - m_tiles(u)[0]), ())))
-            combine(u, 1)
-            tick()
-            if not last:
-                product(u + 1, 1, SIN)
-                tick()
-            quantise(u, 1)
-            make_tables(u, 1)
-            for m in m_tiles(u):
-                queue(multiply(m, 1, fine=STEPS.get((u, 1), STORE_BANKS), vbanks=VB.get((u, 1, m - m_tiles(u)[0]), ())))
-        for item in pending:
-            flush(item[1])
+            if u in GUNITS:
+                for e in (0, 1):
+                    if e == 0:
+                        product(u, 0, COS)
+                    else:
+                        product(u, 1, COS)
+                        product(u, 0, SIN)
+                    flush(later)
+                    later = []
+                    make_tables((u, e))
+                    if waiting is not None:
+                        quantise_g(*waiting)
+                        later = mult(*waiting)
+                    combine_g(u, e)
+                    waiting = (u, e)
+                    if e == 1 and not last:
+                        opt_stage(u + 2)
+                        product(u + 1, 1, SIN)
+            else:
+                product(u, 0, COS)
+                if waiting is not None:
+                    flush(later)
+                    quantise_g(*waiting)
+                    later = mult(*waiting)
+                    waiting = None
+                product(u, 0, SIN)
+                combine(u, 0)
+                product(u, 1, COS)
+                quantise(u, 0)
+                flush(later)
+                later = mult(u, 0)
+                combine(u, 1)
+                make_tables((u, 0))
+                if not last:
+                    opt_stage(u + 2)
+                    product(u + 1, 1, SIN)
+                quantise(u, 1)
+                flush(later)
+                later = mult(u, 1)
+                make_tables((u, 1))
+        flush(later)

@@ -22,7 +22,6 @@ TWO_PI = 2.0 * math.pi
 
 P = 128
 PACK = 4
-assert TOKENS == P * PACK
 
 LOAD_COLS = 512
 LOADS = WIDTH // LOAD_COLS
@@ -38,24 +37,21 @@ FOLDED_PAIRS = 640
 SIN_FOLD_TOKEN = math.pi * ROPE_BASE ** (WRAPPED_PAIRS / PAIRS)
 COS_FOLD_TOKEN = 1.5 * math.pi * ROPE_BASE ** (WRAPPED_PAIRS / PAIRS)
 COS_FOLD_PAIRS = 64
-UNITS = [(640, 128), (768, 128), (896, 128), (512, 128), (0, 128), (128, 128), (256, 128), (384, 128)]
+UNITS = [640, 768, 896, 512, 0, 128, 256, 384]
 G_LOADS = [(640, 128), (768, 256), (512, 128), (0, 256), (256, 256)]
+LATE_LOADS = 5
 S_REGROUPS = (0, 1)
-STORE_BANKS = 2
 SEEDS = 8
 RADIX = 4
-VB = {(7, 0, 0): (1, 3), (7, 1, 0): (1, 3), (1, 1, 0): (3,), (3, 1, 0): (3,), (5, 1, 0): (3,)}
-DELAY = 4
-TABLES_AT = {(1, 0): (3,), (3, 1): (5,), (4, 1): (6,), (5, 1): (7,)}
+RUN = 8
+FW = 4
+STAGED = range(1, 8)
+G_SUMS = set((u, e) for u in range(1, 8) for e in (0, 1) if (u, e) != (7, 1))
+V_BANKS = {(1, 0): (0,), (2, 0): (0,), (3, 0): (0,), (4, 1): (0,), (5, 0): (0,), (5, 1): (0,), (6, 0): (0,), (6, 1): (0,), (7, 0): (0, 2), (7, 1): (1, 3)}
+STORE_STEP = {(6, 0): 4, (6, 1): 4, (7, 0): 4, (7, 1): 4}
 WRAP_A = {(3, 0): (5,), (4, 0): (6,), (5, 0): (7,)}
 WRAP_B = {(3, 1): (5,), (4, 1): (6,), (5, 1): (7,)}
-VG = {(2,0):(0,),(2,1):(0,),(3,0):(0,),(3,1):(0,),(4,0):(0,),(4,1):(0,),(5,0):(0,),(5,1):(0,),(6,0):(0,),(6,1):(0,),(7,0):(1,3),(7,1):(1,3)}
-STAGED = range(2, 7)
-GUNITS = (2, 3, 4, 5, 6)
-HEAD_WRAP = True
-FINE_FROM = 7
-RUN = 8
-STEPS = {(7, 0): 4, (7, 1): 2}
+TABLES = {(1, 0): (3,), (3, 1): (5,), (4, 1): (6,), (5, 1): (7,)}
 
 
 def regroup(copy, grouped, rows):
@@ -75,10 +71,10 @@ def tile_ropeattention_pa_kernel(tc, x, w, grad_out, out):
         keep = stack.enter_context(tc.tile_pool(name="keep", bufs=1))
         angles = stack.enter_context(tc.tile_pool(name="angles", bufs=2))
         work = stack.enter_context(tc.tile_pool(name="work", bufs=2))
+        sums = stack.enter_context(tc.tile_pool(name="sums", bufs=1))
         results = stack.enter_context(tc.tile_pool(name="results", bufs=6))
         banks = stack.enter_context(tc.psum_pool(name="banks", bufs=6))
-        staging = stack.enter_context(tc.psum_pool(name="staging", bufs=2))
-        sums = stack.enter_context(tc.tile_pool(name="sums", bufs=1))
+        staging = stack.enter_context(tc.psum_pool(name="staging", bufs=8 - 6))
         stack.enter_context(tc.manual_schedule())
 
         x_raw = [keep.tile([P, PACK, LOAD_COLS], BF16, name="x_raw%d" % c) for c in range(LOADS)]
@@ -94,11 +90,9 @@ def tile_ropeattention_pa_kernel(tc, x, w, grad_out, out):
             nc.sync.dma_start(out=g_raw[first][:], in_=g_rows[:, :, 2 * first : 2 * (first + pairs)])
 
         load_g(0)
-        load_x(0)
-        load_x(1)
-        load_x(2)
-        load_x(3)
-        for k in range(1, len(G_LOADS)):
+        for c in range(LOADS):
+            load_x(c)
+        for k in range(1, LATE_LOADS):
             load_g(k)
 
         token_int = keep.tile([P, PACK], I32)
@@ -136,29 +130,27 @@ def tile_ropeattention_pa_kernel(tc, x, w, grad_out, out):
                 nc.vector.tensor_scalar(out=token_radians_neg, in0=token[:], scalar1=-TWO_PI, scalar2=None, op0=ALU.mult)
                 nc.vector.tensor_scalar(out=beyond[:, 0, :], in0=token[:], scalar1=SIN_FOLD_TOKEN, scalar2=None, op0=ALU.is_gt)
                 nc.vector.tensor_scalar(out=beyond[:, 1, :], in0=token[:], scalar1=COS_FOLD_TOKEN, scalar2=None, op0=ALU.is_gt)
-        assert filled == M_TILE
         nc.vector.tensor_scalar(out=fold_sign[:], in0=beyond[:], scalar1=-2.0, scalar2=1.0, op0=ALU.mult, op1=ALU.add)
         nc.vector.tensor_scalar(out=fold_bias[:, 0, :], in0=beyond[:, 0, :], scalar1=math.pi, scalar2=None, op0=ALU.mult)
         nc.vector.tensor_scalar(out=fold_bias[:, 1, :], in0=beyond[:, 1, :], scalar1=-TWO_PI, scalar2=math.pi / 2.0, op0=ALU.mult, op1=ALU.add)
-        for first, pairs in UNITS:
-            for block in range(first, first + pairs, M_TILE):
-                if block > 0:
-                    scaled_copy(block, M_TILE)
+        for first in UNITS:
+            if first > 0:
+                scaled_copy(first, M_TILE)
         nc.vector.tensor_tensor(out=fold_scale[:], in0=fold_sign[:], in1=radians[:], op=ALU.mult)
 
         sin_t = keep.tile([P, PACK, PAIRS], F32)
         cos_t = keep.tile([P, PACK, PAIRS], F32)
 
-        def direct_tables(first, pairs):
-            cols = slice(first, first + pairs)
+        def direct_tables(first):
+            cols = slice(first, first + M_TILE)
             for t in range(PACK):
                 nc.scalar.activation(out=sin_t[:, t, cols], in_=turns[:, cols], func=ACT.Sin, scale=token_radians[:, t : t + 1])
                 nc.scalar.activation(out=cos_t[:, t, cols], in_=turns[:, cols], func=ACT.Sin, scale=token_radians_neg[:, t : t + 1], bias=math.pi / 2.0)
 
-        def folded_tables(first, pairs):
-            cols = slice(first, first + pairs)
+        def folded_tables(first):
+            cols = slice(first, first + M_TILE)
             low = slice(first, first + COS_FOLD_PAIRS)
-            high = slice(first + COS_FOLD_PAIRS, first + pairs)
+            high = slice(first + COS_FOLD_PAIRS, first + M_TILE)
             for t in range(PACK):
                 nc.scalar.activation(out=sin_t[:, t, cols], in_=turns[:, cols], func=ACT.Sin, scale=fold_scale[:, 0, t : t + 1], bias=fold_bias[:, 0, t : t + 1])
                 nc.scalar.activation(out=cos_t[:, t, low], in_=turns[:, low], func=ACT.Sin, scale=fold_scale[:, 1, t : t + 1], bias=fold_bias[:, 1, t : t + 1])
@@ -166,32 +158,34 @@ def tile_ropeattention_pa_kernel(tc, x, w, grad_out, out):
 
         wrapped = {}
 
-        def wrap_a(first, pairs):
-            cols = slice(first, first + pairs)
-            whole = angles.tile([P, PACK, pairs], I32, tag="whole")
-            frac = angles.tile([P, PACK, pairs], F32, tag="frac")
+        def wrap_a(u):
+            cols = slice(UNITS[u], UNITS[u] + M_TILE)
+            whole = angles.tile([P, PACK, M_TILE], I32, tag="whole")
+            frac = angles.tile([P, PACK, M_TILE], F32, tag="frac")
             for t in range(PACK):
                 nc.vector.tensor_scalar(out=whole[:, t, :], in0=turns[:, cols], scalar1=token[:, t : t + 1], scalar2=None, op0=ALU.mult)
             for t in range(PACK):
                 nc.vector.scalar_tensor_tensor(out=frac[:, t, :], in0=turns[:, cols], scalar=token[:, t : t + 1], in1=whole[:, t, :], op0=ALU.mult, op1=ALU.subtract)
-            wrapped[first] = frac
+            wrapped[u] = frac
 
-        def wrap_b(first, pairs):
-            frac = wrapped[first]
-            minus_q = angles.tile([P, PACK, pairs], F32, tag="minus_q")
+        def wrap_b(u):
+            frac = wrapped[u]
+            minus_q = angles.tile([P, PACK, M_TILE], F32, tag="minus_q")
             for half in (slice(0, PACK // 2), slice(PACK // 2, PACK)):
                 nc.vector.scalar_tensor_tensor(out=minus_q[:, half, :], in0=frac[:, half, :], scalar=0.25, in1=frac[:, half, :], op0=ALU.is_gt, op1=ALU.subtract)
-            wrapped[first] = (frac, minus_q)
+            wrapped[u] = (frac, minus_q)
 
-        def wrap_sin(first, pairs):
-            cols = slice(first, first + pairs)
-            frac = wrapped[first][0]
-            nc.scalar.activation(out=sin_t[:, :, cols], in_=frac[:], func=ACT.Sin, scale=TWO_PI)
-
-        def wrap_cos(first, pairs):
-            cols = slice(first, first + pairs)
-            minus_q = wrapped[first][1]
-            nc.scalar.activation(out=cos_t[:, :, cols], in_=minus_q[:], func=ACT.Sin, scale=-TWO_PI, bias=math.pi / 2.0)
+        def tables(u):
+            first = UNITS[u]
+            cols = slice(first, first + M_TILE)
+            if first < WRAPPED_PAIRS:
+                frac, minus_q = wrapped[u]
+                nc.scalar.activation(out=sin_t[:, :, cols], in_=frac[:], func=ACT.Sin, scale=TWO_PI)
+                nc.scalar.activation(out=cos_t[:, :, cols], in_=minus_q[:], func=ACT.Sin, scale=-TWO_PI, bias=math.pi / 2.0)
+            elif first < FOLDED_PAIRS:
+                folded_tables(first)
+            else:
+                direct_tables(first)
 
         x_codes = keep.tile([P, WIDTH], U32, align_bytes=64)
         x_scales = keep.tile([P, WIDTH], U8, align_bytes=64)
@@ -207,144 +201,89 @@ def tile_ropeattention_pa_kernel(tc, x, w, grad_out, out):
         gy_codes = keep.tile([P, 2, PAIRS], U32, align_bytes=64)
         gy_scales = keep.tile([P, 2, PAIRS], U8, align_bytes=64)
 
-        open_tiles = {}
+        full = {}
+        result_tiles = {}
 
-        def pass_(m, e, n):
-            n_cols = slice(n * N_TILE, (n + 1) * N_TILE)
-            bank = banks.tile([P, N_TILE], F32)
+        def pass_(u, e, n):
+            rows = slice(UNITS[u], UNITS[u] + M_TILE)
+            cols = slice(n * N_TILE, (n + 1) * N_TILE)
+            bank = banks.tile([P, N_TILE], F32, name="bank")
             nc.tensor.matmul_mx(
-                out=bank[:], lhsT=gy_codes[:, e, m * M_TILE : (m + 1) * M_TILE].bitcast(E5M2_X4), lhsT_scale=gy_scales[:, e, m * M_TILE : (m + 1) * M_TILE],
-                rhs=x_codes[:, n_cols].bitcast(E4M3_X4), rhs_scale=x_scales[:, n_cols], start=True, stop=True,
+                out=bank[:], lhsT=gy_codes[:, e, rows].bitcast(E5M2_X4), lhsT_scale=gy_scales[:, e, rows],
+                rhs=x_codes[:, cols].bitcast(E4M3_X4), rhs_scale=x_scales[:, cols], start=True, stop=True,
             )
-            return bank
+            full[(u, e, n)] = bank
 
-        def empty(m, e, n, bank, engine, store_now):
-            n_cols = slice(n * N_TILE, (n + 1) * N_TILE)
-            if (m, e) not in open_tiles:
-                open_tiles[(m, e)] = results.tile([P, WIDTH], F32, name="result")
-            result = open_tiles[(m, e)]
-            if engine == "V":
-                nc.vector.tensor_copy(out=result[:, n_cols], in_=bank[:])
-            else:
-                nc.scalar.copy(out=result[:, n_cols], in_=bank[:])
-            rows = out_by_parity[e, m * M_TILE : (m + 1) * M_TILE, :]
-            if store_now == 1:
-                nc.sync.dma_start(out=rows[:, n_cols], in_=result[:, n_cols])
-            elif store_now == 4:
-                nc.sync.dma_start(out=rows, in_=result[:])
+        def empty(u, e, n, copy):
+            if (u, e) not in result_tiles:
+                result_tiles[(u, e)] = results.tile([P, WIDTH], F32, name="result")
+            copy(out=result_tiles[(u, e)][:, n * N_TILE : (n + 1) * N_TILE], in_=full[(u, e, n)][:])
 
-        def store(m, e, n0, n1):
+        def store(u, e, n0, n1):
             cols = slice(n0 * N_TILE, n1 * N_TILE)
-            nc.sync.dma_start(out=out_by_parity[e, m * M_TILE : (m + 1) * M_TILE, cols], in_=open_tiles[(m, e)][:, cols])
+            nc.sync.dma_start(out=out_by_parity[e, UNITS[u] : UNITS[u] + M_TILE, cols], in_=result_tiles[(u, e)][:, cols])
 
-        def multiply(m, e, fine=2, vbanks=()):
-            step = fine
-            later = []
+        def multiply(u, e):
             for n in range(N_TILES):
-                bank = pass_(m, e, n)
-                if n in vbanks:
-                    later.append((m, e, n, bank, "V", 0))
-                else:
-                    empty(m, e, n, bank, "S", 0)
-                if (n + 1) % step == 0:
-                    if any(k in vbanks for k in range(n + 1 - step, n + 1)):
-                        later.append((m, e, n + 1 - step, n + 1))
-                    else:
-                        store(m, e, n + 1 - step, n + 1)
-            return later
+                pass_(u, e, n)
+            for n in range(N_TILES):
+                if n not in V_BANKS.get((u, e), ()):
+                    empty(u, e, n, nc.scalar.copy)
 
-        def flush(later):
-            for item in later:
-                if len(item) == 4:
-                    store(*item)
-                else:
-                    empty(*item)
-
-        def by_parity(u):
-            first, pairs = UNITS[u]
-            start = max(f for f, n in G_LOADS if f <= first)
-            return g_raw[start][:, :, 2 * (first - start) : 2 * (first - start + pairs)].rearrange("p t (i e) -> p e t i", e=2)
+        def finish(u, e):
+            for n in V_BANKS.get((u, e), ()):
+                empty(u, e, n, nc.vector.tensor_copy)
+            step = STORE_STEP.get((u, e), 2)
+            for n in range(0, N_TILES, step):
+                store(u, e, n, n + step)
 
         SIN, COS = 0, 1
         terms = {}
-        groupeds = {}
+        grouped = {}
+        g_pairs = {}
 
-        staged = {}
+        def loaded(u):
+            start = max(f for f, n in G_LOADS if f <= UNITS[u])
+            return g_raw[start][:, :, 2 * (UNITS[u] - start) : 2 * (UNITS[u] - start + M_TILE)]
 
         def stage(u):
-            first, pairs = UNITS[u]
-            start = max(f for f, n in G_LOADS if f <= first)
-            cols = slice(2 * (first - start), 2 * (first - start + pairs))
-            bank = staging.tile([P, PACK, 2 * pairs], BF16, name="staged")
+            bank = staging.tile([P, PACK, 2 * M_TILE], BF16, name="staged")
             for half in (slice(0, PACK // 2), slice(PACK // 2, PACK)):
-                nc.tensor.matmul(bank[:, half, :], lhsT=identity[:], rhs=g_raw[start][:, half, cols], start=True, stop=True)
-            staged[u] = bank[:].rearrange("p t (i e) -> p e t i", e=2)
+                nc.tensor.matmul(bank[:, half, :], lhsT=identity[:], rhs=loaded(u)[:, half, :], start=True, stop=True)
+            g_pairs[u] = bank[:].rearrange("p t (i e) -> p e t i", e=2)
 
         def product(u, e, table):
-            first, pairs = UNITS[u]
-            term = work.tile([P, PACK, pairs], F32, tag="term_%d_%d" % (e, table))
-            g_pairs = staged[u] if u in staged else by_parity(u)
-            nc.vector.tensor_tensor(out=term[:], in0=g_pairs[:, e], in1=(sin_t, cos_t)[table][:, :, first : first + pairs], op=ALU.mult)
+            if u not in g_pairs:
+                g_pairs[u] = loaded(u).rearrange("p t (i e) -> p e t i", e=2)
+            term = work.tile([P, PACK, M_TILE], F32, tag="term_%d_%d" % (e, table))
+            nc.vector.tensor_tensor(out=term[:], in0=g_pairs[u][:, e], in1=(sin_t, cos_t)[table][:, :, UNITS[u] : UNITS[u] + M_TILE], op=ALU.mult)
             terms[(u, e, table)] = term
 
         def combine(u, e):
-            first, pairs = UNITS[u]
-            if u not in groupeds:
-                groupeds[u] = work.tile([P, 2, pairs, PACK], BF16, align_bytes=64, name="grouped")
-            nc.vector.tensor_tensor(
-                out=groupeds[u][:, e].rearrange("p (c i) t -> p c t i", i=4),
+            on_g = (u, e) in G_SUMS
+            pool = sums if on_g else work
+            tile = pool.tile([P, M_TILE, PACK], BF16, align_bytes=64, name="summed" if on_g else "grouped%d" % e)
+            (nc.gpsimd if on_g else nc.vector).tensor_tensor(
+                out=tile[:].rearrange("p (c i) t -> p c t i", i=4),
                 in0=terms[(u, e, COS)][:].rearrange("p t (c i) -> p c t i", i=4),
                 in1=terms[(u, 1 - e, SIN)][:].rearrange("p t (c i) -> p c t i", i=4),
                 op=(ALU.add if e == 0 else ALU.subtract),
             )
-
-        def combine_g(u, e):
-            first, pairs = UNITS[u]
-            grouped = sums.tile([P, pairs, PACK], BF16, align_bytes=64, name="summed")
-            nc.gpsimd.tensor_tensor(
-                out=grouped[:].rearrange("p (c i) t -> p c t i", i=4),
-                in0=terms[(u, e, COS)][:].rearrange("p t (c i) -> p c t i", i=4),
-                in1=terms[(u, 1 - e, SIN)][:].rearrange("p t (c i) -> p c t i", i=4),
-                op=(ALU.add if e == 0 else ALU.subtract),
-            )
-            summed[(u, e)] = grouped
-
-        summed = {}
-
-        def quantise_g(u, e):
-            first, pairs = UNITS[u]
-            nc.vector.quantize_mx(out=gy_codes[:, e, first : first + pairs].bitcast(E5M2_X4), scales=gy_scales[:, e, first : first + pairs], in_=summed[(u, e)][:].rearrange("p c t -> p (c t)"))
+            grouped[(u, e)] = tile
 
         def quantise(u, e):
-            first, pairs = UNITS[u]
-            nc.vector.quantize_mx(out=gy_codes[:, e, first : first + pairs].bitcast(E5M2_X4), scales=gy_scales[:, e, first : first + pairs], in_=groupeds[u][:, e].rearrange("p c t -> p (c t)"))
+            cols = slice(UNITS[u], UNITS[u] + M_TILE)
+            nc.vector.quantize_mx(out=gy_codes[:, e, cols].bitcast(E5M2_X4), scales=gy_scales[:, e, cols], in_=grouped[(u, e)][:].rearrange("p c t -> p (c t)"))
 
-        def m_tiles(u):
-            first, pairs = UNITS[u]
-            return range(first // M_TILE, (first + pairs) // M_TILE)
+        def first_banks(n):
+            for e in (0, 1):
+                pass_(0, e, n)
+                empty(0, e, n, nc.scalar.copy)
+                store(0, e, n, n + 1)
 
-        def tables_v(u):
-            first, pairs = UNITS[u]
-            if first < WRAPPED_PAIRS:
-                wrap_a(first, pairs)
-                wrap_b(first, pairs)
-
-        def tables_s(u):
-            first, pairs = UNITS[u]
-            if first < WRAPPED_PAIRS:
-                wrap_sin(first, pairs)
-                wrap_cos(first, pairs)
-            elif first < FOLDED_PAIRS:
-                folded_tables(first, pairs)
-            else:
-                direct_tables(first, pairs)
-
-        m0 = UNITS[0][0] // M_TILE
-        tables_s(0)
-        tables_s(1)
-        FW = min(u for u in range(len(UNITS)) if UNITS[u][0] < WRAPPED_PAIRS)
-        if HEAD_WRAP:
-            wrap_a(*UNITS[FW])
+        tables(0)
+        tables(1)
+        wrap_a(FW)
         x_regroup(0)
         product(0, 1, SIN)
         product(0, 0, COS)
@@ -353,89 +292,52 @@ def tile_ropeattention_pa_kernel(tc, x, w, grad_out, out):
         product(0, 1, COS)
         quantise(0, 0)
         x_regroup(1)
-        tables_s(2)
+        tables(2)
         combine(0, 1)
-        wrap_b(*UNITS[FW])
+        wrap_b(FW)
         x_quantise(0)
-        b = pass_(m0, 0, 0)
+        pass_(0, 0, 0)
         quantise(0, 1)
         x_regroup(2)
-        empty(m0, 0, 0, b, "S", 1)
-        b = pass_(m0, 1, 0)
-        empty(m0, 1, 0, b, "S", 1)
+        empty(0, 0, 0, nc.scalar.copy)
+        store(0, 0, 0, 1)
+        pass_(0, 1, 0)
+        empty(0, 1, 0, nc.scalar.copy)
+        store(0, 1, 0, 1)
         x_quantise(1)
         x_regroup(3)
         x_quantise(2)
-        for n in (1, 2):
-            for e in (0, 1):
-                b = pass_(m0, e, n)
-                empty(m0, e, n, b, "S", 1)
+        first_banks(1)
+        stage(1)
+        first_banks(2)
         stage(2)
         x_quantise(3)
-        for e in (0, 1):
-            b = pass_(m0, e, 3)
-            empty(m0, e, 3, b, "S", 1)
-        product(1, 1, SIN)
-        if HEAD_WRAP:
-            tables_s(FW)
+        first_banks(3)
+        for k in range(LATE_LOADS, len(G_LOADS)):
+            load_g(k)
+        tables(FW)
 
-        def make_tables(where):
-            for j in WRAP_A.get(where, ()):
-                wrap_a(*UNITS[j])
-            for j in WRAP_B.get(where, ()):
-                wrap_b(*UNITS[j])
-            for j in TABLES_AT.get(where, ()):
-                tables_s(j)
-
-        def mult(u, e):
-            return multiply(UNITS[u][0] // M_TILE, e, fine=STEPS.get((u, e), STORE_BANKS), vbanks=VG.get((u, e), ()))
-
-        def opt_stage(u):
-            if u in STAGED:
-                stage(u)
-
-        later = []
-        waiting = None
-        for u in range(1, len(UNITS)):
-            last = u == len(UNITS) - 1
-            if u in GUNITS:
-                for e in (0, 1):
-                    if e == 0:
-                        product(u, 0, COS)
-                    else:
-                        product(u, 1, COS)
-                        product(u, 0, SIN)
-                    flush(later)
-                    later = []
-                    make_tables((u, e))
-                    if waiting is not None:
-                        quantise_g(*waiting)
-                        later = mult(*waiting)
-                    combine_g(u, e)
-                    waiting = (u, e)
-                    if e == 1 and not last:
-                        opt_stage(u + 2)
-                        product(u + 1, 1, SIN)
-            else:
-                product(u, 0, COS)
-                if waiting is not None:
-                    flush(later)
-                    quantise_g(*waiting)
-                    later = mult(*waiting)
-                    waiting = None
-                product(u, 0, SIN)
-                combine(u, 0)
-                product(u, 1, COS)
-                quantise(u, 0)
-                flush(later)
-                later = mult(u, 0)
-                combine(u, 1)
-                make_tables((u, 0))
-                if not last:
-                    opt_stage(u + 2)
-                    product(u + 1, 1, SIN)
-                quantise(u, 1)
-                flush(later)
-                later = mult(u, 1)
-                make_tables((u, 1))
-        flush(later)
+        halves = [(u, e) for u in range(1, len(UNITS)) for e in (0, 1)]
+        made = []
+        for k, (u, e) in enumerate(halves):
+            product(u, 1 - e, SIN)
+            product(u, e, COS)
+            if e == 0 and u + 1 in STAGED and u >= 2:
+                stage(u + 1)
+            if len(made) > 1:
+                finish(*made[-2])
+            for j in WRAP_A.get((u, e), ()):
+                wrap_a(j)
+            for j in WRAP_B.get((u, e), ()):
+                wrap_b(j)
+            if made:
+                quantise(*made[-1])
+                multiply(*made[-1])
+            for j in TABLES.get((u, e), ()):
+                tables(j)
+            combine(u, e)
+            made.append((u, e))
+        finish(*made[-2])
+        quantise(*made[-1])
+        multiply(*made[-1])
+        finish(*made[-1])

@@ -48,10 +48,10 @@ FW = 4
 STAGED = range(1, 8)
 G_SUMS = set((u, e) for u in range(1, 8) for e in (0, 1) if (u, e) != (7, 1))
 V_BANKS = {(1, 0): (0,), (2, 0): (0,), (3, 0): (0,), (4, 1): (0,), (5, 0): (0,), (5, 1): (0,), (6, 0): (0,), (6, 1): (0,), (7, 0): (0, 2), (7, 1): (1, 3)}
-STORE_STEP = {(6, 0): 4, (6, 1): 4, (7, 0): 4, (7, 1): 4}
-WRAP_A = {(3, 0): (5,), (4, 0): (6,), (5, 0): (7,)}
-WRAP_B = {(3, 1): (5,), (4, 1): (6,), (5, 1): (7,)}
-TABLES = {(1, 0): (3,), (3, 1): (5,), (4, 1): (6,), (5, 1): (7,)}
+STORE_STEP = {(6, 1): 4, (7, 0): 4, (7, 1): 4}
+WRAP_A = {(3, 1): (5,), (4, 1): (6,), (5, 1): (7,)}
+WRAP_B = {(4, 0): (5,), (5, 0): (6,), (6, 0): (7,)}
+TABLES = {(1, 0): (3,), (4, 0): (5,), (5, 0): (6,), (6, 0): (7,)}
 
 
 def regroup(copy, grouped, rows):
@@ -138,11 +138,13 @@ def tile_ropeattention_pa_kernel(tc, x, w, grad_out, out):
                 scaled_copy(first, M_TILE)
         nc.vector.tensor_tensor(out=fold_scale[:], in0=fold_sign[:], in1=radians[:], op=ALU.mult)
 
-        sin_t = keep.tile([P, PACK, PAIRS], F32)
-        cos_t = keep.tile([P, PACK, PAIRS], F32)
+        COS, SIN = 0, 1
+        trig = keep.tile([P, 2, PACK, PAIRS], F32)
+        cos_t = trig[:, COS]
+        sin_t = trig[:, SIN]
 
-        def direct_tables(first):
-            cols = slice(first, first + M_TILE)
+        def direct_tables(first, pairs):
+            cols = slice(first, first + pairs)
             for t in range(PACK):
                 nc.scalar.activation(out=sin_t[:, t, cols], in_=turns[:, cols], func=ACT.Sin, scale=token_radians[:, t : t + 1])
                 nc.scalar.activation(out=cos_t[:, t, cols], in_=turns[:, cols], func=ACT.Sin, scale=token_radians_neg[:, t : t + 1], bias=math.pi / 2.0)
@@ -171,8 +173,7 @@ def tile_ropeattention_pa_kernel(tc, x, w, grad_out, out):
         def wrap_b(u):
             frac = wrapped[u]
             minus_q = angles.tile([P, PACK, M_TILE], F32, tag="minus_q")
-            for half in (slice(0, PACK // 2), slice(PACK // 2, PACK)):
-                nc.vector.scalar_tensor_tensor(out=minus_q[:, half, :], in0=frac[:, half, :], scalar=0.25, in1=frac[:, half, :], op0=ALU.is_gt, op1=ALU.subtract)
+            nc.vector.scalar_tensor_tensor(out=minus_q[:], in0=frac[:], scalar=0.25, in1=frac[:], op0=ALU.is_gt, op1=ALU.subtract)
             wrapped[u] = (frac, minus_q)
 
         def tables(u):
@@ -185,7 +186,7 @@ def tile_ropeattention_pa_kernel(tc, x, w, grad_out, out):
             elif first < FOLDED_PAIRS:
                 folded_tables(first)
             else:
-                direct_tables(first)
+                direct_tables(first, M_TILE)
 
         x_codes = keep.tile([P, WIDTH], U32, align_bytes=64)
         x_scales = keep.tile([P, WIDTH], U8, align_bytes=64)
@@ -237,7 +238,6 @@ def tile_ropeattention_pa_kernel(tc, x, w, grad_out, out):
             for n in range(0, N_TILES, step):
                 store(u, e, n, n + step)
 
-        SIN, COS = 0, 1
         terms = {}
         grouped = {}
         g_pairs = {}
@@ -252,21 +252,22 @@ def tile_ropeattention_pa_kernel(tc, x, w, grad_out, out):
                 nc.tensor.matmul(bank[:, half, :], lhsT=identity[:], rhs=loaded(u)[:, half, :], start=True, stop=True)
             g_pairs[u] = bank[:].rearrange("p t (i e) -> p e t i", e=2)
 
-        def product(u, e, table):
+        def products(u, e):
             if u not in g_pairs:
                 g_pairs[u] = loaded(u).rearrange("p t (i e) -> p e t i", e=2)
-            term = work.tile([P, PACK, M_TILE], F32, tag="term_%d_%d" % (e, table))
-            nc.vector.tensor_tensor(out=term[:], in0=g_pairs[u][:, e], in1=(sin_t, cos_t)[table][:, :, UNITS[u] : UNITS[u] + M_TILE], op=ALU.mult)
-            terms[(u, e, table)] = term
+            term = work.tile([P, 2, PACK, M_TILE], F32, tag="term%d" % e)
+            factors = trig[:, :, :, UNITS[u] : UNITS[u] + M_TILE] if e == 0 else trig[:, ::-1, :, UNITS[u] : UNITS[u] + M_TILE]
+            nc.vector.tensor_tensor(out=term[:], in0=g_pairs[u], in1=factors, op=ALU.mult)
+            terms[(u, e)] = term
 
         def combine(u, e):
             on_g = (u, e) in G_SUMS
             pool = sums if on_g else work
             tile = pool.tile([P, M_TILE, PACK], BF16, align_bytes=64, name="summed" if on_g else "grouped%d" % e)
+            runs = terms[(u, e)][:].rearrange("p k t (c i) -> p k c t i", i=4)
             (nc.gpsimd if on_g else nc.vector).tensor_tensor(
                 out=tile[:].rearrange("p (c i) t -> p c t i", i=4),
-                in0=terms[(u, e, COS)][:].rearrange("p t (c i) -> p c t i", i=4),
-                in1=terms[(u, 1 - e, SIN)][:].rearrange("p t (c i) -> p c t i", i=4),
+                in0=runs[:, e], in1=runs[:, 1 - e],
                 op=(ALU.add if e == 0 else ALU.subtract),
             )
             grouped[(u, e)] = tile
@@ -285,16 +286,14 @@ def tile_ropeattention_pa_kernel(tc, x, w, grad_out, out):
         tables(1)
         wrap_a(FW)
         x_regroup(0)
-        product(0, 1, SIN)
-        product(0, 0, COS)
-        product(0, 0, SIN)
+        products(0, 0)
+        wrap_b(FW)
         combine(0, 0)
-        product(0, 1, COS)
+        products(0, 1)
         quantise(0, 0)
         x_regroup(1)
         tables(2)
         combine(0, 1)
-        wrap_b(FW)
         x_quantise(0)
         pass_(0, 0, 0)
         quantise(0, 1)
@@ -319,9 +318,8 @@ def tile_ropeattention_pa_kernel(tc, x, w, grad_out, out):
 
         halves = [(u, e) for u in range(1, len(UNITS)) for e in (0, 1)]
         made = []
-        for k, (u, e) in enumerate(halves):
-            product(u, 1 - e, SIN)
-            product(u, e, COS)
+        for u, e in halves:
+            products(u, e)
             if e == 0 and u + 1 in STAGED and u >= 2:
                 stage(u + 1)
             if len(made) > 1:
@@ -332,9 +330,10 @@ def tile_ropeattention_pa_kernel(tc, x, w, grad_out, out):
                 wrap_b(j)
             if made:
                 quantise(*made[-1])
-                multiply(*made[-1])
             for j in TABLES.get((u, e), ()):
                 tables(j)
+            if made:
+                multiply(*made[-1])
             combine(u, e)
             made.append((u, e))
         finish(*made[-2])

@@ -51,7 +51,8 @@ V_BANKS = {(1, 0): (0,), (2, 0): (0,), (3, 0): (0,), (4, 1): (0,), (5, 0): (0,),
 STORE_STEP = {(6, 1): 4, (7, 0): 4, (7, 1): 4}
 WRAP_A = {(3, 1): (5,), (4, 1): (6,), (5, 1): (7,)}
 WRAP_B = {(4, 0): (5,), (5, 0): (6,), (6, 0): (7,)}
-TABLES = {(1, 0): (3,), (4, 0): (5,), (5, 0): (6,), (6, 0): (7,)}
+TABLES = {(4, 0): (5,), (5, 0): (6,), (6, 0): (7,)}
+TABLES_LATER = {}
 
 
 def regroup(copy, grouped, rows):
@@ -195,6 +196,21 @@ def tile_ropeattention_pa_kernel(tc, x, w, grad_out, out):
         def x_regroup(c):
             regroup(nc.scalar.copy if c in S_REGROUPS else nc.vector.tensor_copy, x_grouped[c][:], x_raw[c][:])
 
+        def x_regroup_pe(c, half):
+            half_cols = LOAD_COLS // 2
+            bank = staging.tile([P, half_cols, PACK], BF16, name="staged")
+            for q in (0, 1):
+                cols = slice(half * half_cols + q * M_TILE, half * half_cols + (q + 1) * M_TILE)
+                nc.tensor.matmul(
+                    bank[:, q * M_TILE : (q + 1) * M_TILE, :].rearrange("p (c i) t -> p c t i", i=RUN), lhsT=identity[:],
+                    rhs=x_raw[c][:, :, cols].rearrange("p t (c i) -> p c t i", i=RUN), start=True, stop=True,
+                )
+            return bank
+
+        def x_collect(c, half, bank):
+            half_cols = LOAD_COLS // 2
+            nc.scalar.copy(out=x_grouped[c][:, half * half_cols : (half + 1) * half_cols, :], in_=bank[:])
+
         def x_quantise(c):
             cols = slice(c * LOAD_COLS, (c + 1) * LOAD_COLS)
             nc.vector.quantize_mx(out=x_codes[:, cols].bitcast(E4M3_X4), scales=x_scales[:, cols], in_=x_grouped[c][:].rearrange("p c t -> p (c t)"))
@@ -291,16 +307,19 @@ def tile_ropeattention_pa_kernel(tc, x, w, grad_out, out):
         combine(0, 0)
         products(0, 1)
         quantise(0, 0)
-        x_regroup(1)
-        tables(2)
+        x_first = x_regroup_pe(1, 0)
+        x_second = x_regroup_pe(1, 1)
+        x_collect(1, 0, x_first)
         combine(0, 1)
         x_quantise(0)
         pass_(0, 0, 0)
         quantise(0, 1)
+        pass_(0, 1, 0)
         x_regroup(2)
+        x_collect(1, 1, x_second)
+        tables(2)
         empty(0, 0, 0, nc.scalar.copy)
         store(0, 0, 0, 1)
-        pass_(0, 1, 0)
         empty(0, 1, 0, nc.scalar.copy)
         store(0, 1, 0, 1)
         x_quantise(1)
@@ -310,6 +329,7 @@ def tile_ropeattention_pa_kernel(tc, x, w, grad_out, out):
         stage(1)
         first_banks(2)
         stage(2)
+        tables(3)
         x_quantise(3)
         first_banks(3)
         for k in range(LATE_LOADS, len(G_LOADS)):
@@ -334,9 +354,11 @@ def tile_ropeattention_pa_kernel(tc, x, w, grad_out, out):
                 tables(j)
             if made:
                 multiply(*made[-1])
+            for j in TABLES_LATER.get((u, e), ()):
+                tables(j)
             combine(u, e)
             made.append((u, e))
-        finish(*made[-2])
         quantise(*made[-1])
         multiply(*made[-1])
+        finish(*made[-2])
         finish(*made[-1])

@@ -46,7 +46,8 @@ RADIX = 4
 RUN = 8
 FW = 4
 STAGED = range(1, 8)
-G_SUMS = set((u, e) for u in range(1, 8) for e in (0, 1) if (u, e) != (7, 1))
+G_SUMS = set((u, e) for u in range(1, 8) for e in (0, 1) if (u, e) != (7, 1) and not (u in (1,) and e == 1))
+MIXED = (1,)
 V_BANKS = {(1, 0): (0,), (2, 0): (0,), (3, 0): (0,), (4, 1): (0,), (5, 0): (0,), (5, 1): (0,), (6, 0): (0,), (6, 1): (0,), (7, 0): (0, 2), (7, 1): (1, 3)}
 STORE_STEP = {(6, 1): 4, (7, 0): 4, (7, 1): 4}
 WRAP_A = {(3, 1): (5,), (4, 1): (6,), (5, 1): (7,)}
@@ -272,8 +273,12 @@ def tile_ropeattention_pa_kernel(tc, x, w, grad_out, out):
             if u not in g_pairs:
                 g_pairs[u] = loaded(u).rearrange("p t (i e) -> p e t i", e=2)
             term = work.tile([P, 2, PACK, M_TILE], F32, tag="term%d" % e)
-            factors = trig[:, :, :, UNITS[u] : UNITS[u] + M_TILE] if e == 0 else trig[:, ::-1, :, UNITS[u] : UNITS[u] + M_TILE]
-            nc.vector.tensor_tensor(out=term[:], in0=g_pairs[u], in1=factors, op=ALU.mult)
+            factors = trig[:, :, :, UNITS[u] : UNITS[u] + M_TILE]
+            if e == 0:
+                nc.vector.tensor_tensor(out=term[:], in0=g_pairs[u], in1=factors, op=ALU.mult)
+            else:
+                for k in (0, 1):
+                    nc.vector.tensor_tensor(out=term[:, k], in0=g_pairs[u][:, k], in1=factors[:, 1 - k], op=ALU.mult)
             terms[(u, e)] = term
 
         def combine(u, e):
@@ -336,29 +341,67 @@ def tile_ropeattention_pa_kernel(tc, x, w, grad_out, out):
             load_g(k)
         tables(FW)
 
-        halves = [(u, e) for u in range(1, len(UNITS)) for e in (0, 1)]
-        made = []
-        for u, e in halves:
-            products(u, e)
-            if e == 0 and u + 1 in STAGED and u >= 2:
+        unquantised = None
+        unfinished = []
+
+        def close(half):
+            quantise(*half)
+            multiply(*half)
+            unfinished.append(half)
+
+        def finish_all(count):
+            for half in unfinished[:count]:
+                finish(*half)
+            for half in list(unfinished[:count]):
+                unfinished.remove(half)
+
+        for u in range(1, len(UNITS)):
+            if u + 1 in STAGED and u >= 2:
                 stage(u + 1)
-            if len(made) > 1:
-                finish(*made[-2])
-            for j in WRAP_A.get((u, e), ()):
-                wrap_a(j)
-            for j in WRAP_B.get((u, e), ()):
-                wrap_b(j)
-            if made:
-                quantise(*made[-1])
-            for j in TABLES.get((u, e), ()):
-                tables(j)
-            if made:
-                multiply(*made[-1])
-            for j in TABLES_LATER.get((u, e), ()):
-                tables(j)
-            combine(u, e)
-            made.append((u, e))
-        quantise(*made[-1])
-        multiply(*made[-1])
-        finish(*made[-2])
-        finish(*made[-1])
+            if u in MIXED:
+                products(u, 0)
+                if unquantised:
+                    close(unquantised)
+                    unquantised = None
+                combine(u, 0)
+                products(u, 1)
+                finish_all(len(unfinished))
+                for e in (0, 1):
+                    for j in WRAP_A.get((u, e), ()):
+                        wrap_a(j)
+                    for j in WRAP_B.get((u, e), ()):
+                        wrap_b(j)
+                combine(u, 1)
+                quantise(u, 0)
+                for e in (0, 1):
+                    for j in TABLES.get((u, e), ()):
+                        tables(j)
+                multiply(u, 0)
+                quantise(u, 1)
+                multiply(u, 1)
+                for e in (0, 1):
+                    for j in TABLES_LATER.get((u, e), ()):
+                        tables(j)
+                unfinished.extend([(u, 0), (u, 1)])
+            else:
+                for e in (0, 1):
+                    products(u, e)
+                    finish_all(len(unfinished))
+                    for j in WRAP_A.get((u, e), ()):
+                        wrap_a(j)
+                    for j in WRAP_B.get((u, e), ()):
+                        wrap_b(j)
+                    if unquantised:
+                        quantise(*unquantised)
+                    for j in TABLES.get((u, e), ()):
+                        tables(j)
+                    if unquantised:
+                        multiply(*unquantised)
+                        unfinished.append(unquantised)
+                    for j in TABLES_LATER.get((u, e), ()):
+                        tables(j)
+                    combine(u, e)
+                    unquantised = (u, e)
+        if unquantised:
+            close(unquantised)
+        finish_all(len(unfinished))

@@ -38,8 +38,8 @@ SIN_FOLD_TOKEN = math.pi * ROPE_BASE ** (WRAPPED_PAIRS / PAIRS)
 COS_FOLD_TOKEN = 1.5 * math.pi * ROPE_BASE ** (WRAPPED_PAIRS / PAIRS)
 COS_FOLD_PAIRS = 64
 UNITS = [640, 768, 896, 512, 0, 128, 256, 384]
-G_LOADS = [(640, 128), (768, 256), (512, 128), (0, 256), (256, 256)]
-LATE_LOADS = 5
+G_LOADS = [(640, 128), (768, 256), (512, 128), (0, 512)]
+LATE_LOADS = 4
 S_REGROUPS = (0, 1)
 SEEDS = 8
 RADIX = 4
@@ -49,7 +49,7 @@ STAGED = range(1, 8)
 G_SUMS = set((u, e) for u in range(1, 8) for e in (0, 1) if (u, e) != (7, 1) and not (u in (1,) and e == 1))
 MIXED = (1,)
 V_BANKS = {(1, 0): (0,), (2, 0): (0,), (3, 0): (0,), (4, 1): (0,), (5, 0): (0,), (5, 1): (0,), (6, 0): (0,), (6, 1): (0,), (7, 0): (0, 2), (7, 1): (1, 3)}
-STORE_STEP = {(6, 1): 4, (7, 0): 4, (7, 1): 4}
+STORE_STEP = {(4, 0): 4, (4, 1): 4, (5, 0): 4, (5, 1): 4, (6, 0): 4, (6, 1): 4, (7, 0): 4, (7, 1): 4}
 WRAP_A = {(3, 1): (5,), (4, 1): (6,), (5, 1): (7,)}
 WRAP_B = {(4, 0): (5,), (5, 0): (6,), (6, 0): (7,)}
 TABLES = {(4, 0): (5,), (5, 0): (6,), (6, 0): (7,)}

import math
from contextlib import ExitStack

import concourse.mybir as mybir
from concourse.masks import make_identity

F32 = mybir.dt.float32
BF16 = mybir.dt.bfloat16
I32 = mybir.dt.int32
U32 = mybir.dt.uint32
U8 = mybir.dt.uint8
E4M3_X4 = mybir.dt.float8_e4m3fn_x4
E5M2_X4 = mybir.dt.float8_e5m2_x4
ALU = mybir.AluOpType
ACT = mybir.ActivationFunctionType

TOKENS = 512
WIDTH = 2048
PAIRS = WIDTH // 2
ROPE_BASE = 10000.0
TWO_PI = 2.0 * math.pi

P = 128
PACK = 4

LOAD_COLS = 512
LOADS = WIDTH // LOAD_COLS
M_TILE = 128
N_TILE = 512
N_TILES = WIDTH // N_TILE

FLOPS = 2 * TOKENS * WIDTH * WIDTH
BYTES = 2 * (TOKENS * WIDTH * 2) + WIDTH * WIDTH * 4

WRAPPED_PAIRS = 512
FOLDED_PAIRS = 640
SIN_FOLD_TOKEN = math.pi * ROPE_BASE ** (WRAPPED_PAIRS / PAIRS)
COS_FOLD_TOKEN = 1.5 * math.pi * ROPE_BASE ** (WRAPPED_PAIRS / PAIRS)
COS_FOLD_PAIRS = 64
UNITS = [640, 768, 896, 512, 0, 128, 256, 384]
G_LOADS = [(640, 128), (768, 256), (512, 128), (0, 512)]
LATE_LOADS = 4
S_REGROUPS = (0, 1)
SEEDS = 8
RADIX = 4
RUN = 8
FW = 4
STAGED = range(1, 8)
G_SUMS = set((u, e) for u in range(1, 8) for e in (0, 1) if (u, e) != (7, 1) and not (u in (1,) and e == 1))
MIXED = (1,)
V_BANKS = {(1, 0): (0,), (2, 0): (0,), (3, 0): (0,), (4, 1): (0,), (5, 0): (0,), (5, 1): (0,), (6, 0): (0,), (6, 1): (0,), (7, 0): (0, 2), (7, 1): (1, 3)}
STORE_STEP = {(4, 0): 4, (4, 1): 4, (5, 0): 4, (5, 1): 4, (6, 0): 4, (6, 1): 4, (7, 0): 4, (7, 1): 4}
WRAP_A = {(3, 1): (5,), (4, 1): (6,), (5, 1): (7,)}
WRAP_B = {(4, 0): (5,), (5, 0): (6,), (6, 0): (7,)}
TABLES = {(4, 0): (5,), (5, 0): (6,), (6, 0): (7,)}
TABLES_LATER = {}


def regroup(copy, grouped, rows):
    copy(
        out=grouped.rearrange("p (c i) t -> p c t i", i=RUN),
        in_=rows.rearrange("p t (c i) -> p c t i", i=RUN),
    )


def tile_ropeattention_pa_kernel(tc, x, w, grad_out, out):
    nc = tc.nc
    x_rows = x.rearrange("(p t) c -> p t c", t=PACK)
    g_rows = grad_out.rearrange("(p t) c -> p t c", t=PACK)
    out_by_parity = out.rearrange("(i e) c -> e i c", e=2)

    with ExitStack() as stack:
        keep = stack.enter_context(tc.tile_pool(name="keep", bufs=1))
        angles = stack.enter_context(tc.tile_pool(name="angles", bufs=2))
        work = stack.enter_context(tc.tile_pool(name="work", bufs=2))
        sums = stack.enter_context(tc.tile_pool(name="sums", bufs=1))
        results = stack.enter_context(tc.tile_pool(name="results", bufs=6))
        banks = stack.enter_context(tc.psum_pool(name="banks", bufs=6))
        staging = stack.enter_context(tc.psum_pool(name="staging", bufs=8 - 6))
        stack.enter_context(tc.manual_schedule())

        x_raw = [keep.tile([P, PACK, LOAD_COLS], BF16, name="x_raw%d" % c) for c in range(LOADS)]
        g_raw = {}
        for first, pairs in G_LOADS:
            g_raw[first] = keep.tile([P, PACK, 2 * pairs], BF16, name="g_raw%d" % first)

        def load_x(c):
            nc.sync.dma_start(out=x_raw[c][:], in_=x_rows[:, :, c * LOAD_COLS : (c + 1) * LOAD_COLS])

        def load_g(k):
            first, pairs = G_LOADS[k]
            nc.sync.dma_start(out=g_raw[first][:], in_=g_rows[:, :, 2 * first : 2 * (first + pairs)])

        load_g(0)
        for c in range(LOADS):
            load_x(c)
        for k in range(1, LATE_LOADS):
            load_g(k)

        token_int = keep.tile([P, PACK], I32)
        nc.gpsimd.iota(out=token_int[:], pattern=[[1, PACK]], base=0, channel_multiplier=PACK)
        identity = keep.tile([P, P], BF16)
        make_identity(nc, identity[:])
        one = keep.tile([P, 1], F32)
        nc.vector.memset(one[:], 1.0)
        turns = keep.tile([P, PAIRS], F32)
        token = keep.tile([P, PACK], F32)
        radians = keep.tile([P, 2, PACK], F32)
        token_radians = radians[:, 0, :]
        token_radians_neg = radians[:, 1, :]
        beyond = keep.tile([P, 2, PACK], F32)
        fold_sign = keep.tile([P, 2, PACK], F32)
        fold_scale = keep.tile([P, 2, PACK], F32)
        fold_bias = keep.tile([P, 2, PACK], F32)

        def scaled_copy(first, source_pairs):
            nc.vector.tensor_scalar(
                out=turns[:, first : first + source_pairs], in0=turns[:, 0:source_pairs],
                scalar1=ROPE_BASE ** (-first / PAIRS), scalar2=None, op0=ALU.mult,
            )

        for i in range(SEEDS):
            nc.vector.tensor_scalar(out=turns[:, i : i + 1], in0=one[:], scalar1=ROPE_BASE ** (-i / PAIRS) / TWO_PI, scalar2=None, op0=ALU.mult)
        nc.vector.tensor_copy(out=token[:], in_=token_int[:])
        filled = SEEDS
        while filled < M_TILE:
            for k in range(1, RADIX):
                scaled_copy(k * filled, filled)
            filled *= RADIX
            if filled == SEEDS * RADIX:
                nc.vector.tensor_scalar(out=token_radians, in0=token[:], scalar1=TWO_PI, scalar2=None, op0=ALU.mult)
                nc.vector.tensor_scalar(out=token_radians_neg, in0=token[:], scalar1=-TWO_PI, scalar2=None, op0=ALU.mult)
                nc.vector.tensor_scalar(out=beyond[:, 0, :], in0=token[:], scalar1=SIN_FOLD_TOKEN, scalar2=None, op0=ALU.is_gt)
                nc.vector.tensor_scalar(out=beyond[:, 1, :], in0=token[:], scalar1=COS_FOLD_TOKEN, scalar2=None, op0=ALU.is_gt)
        nc.vector.tensor_scalar(out=fold_sign[:], in0=beyond[:], scalar1=-2.0, scalar2=1.0, op0=ALU.mult, op1=ALU.add)
        nc.vector.tensor_scalar(out=fold_bias[:, 0, :], in0=beyond[:, 0, :], scalar1=math.pi, scalar2=None, op0=ALU.mult)
        nc.vector.tensor_scalar(out=fold_bias[:, 1, :], in0=beyond[:, 1, :], scalar1=-TWO_PI, scalar2=math.pi / 2.0, op0=ALU.mult, op1=ALU.add)
        for first in UNITS:
            if first > 0:
                scaled_copy(first, M_TILE)
        nc.vector.tensor_tensor(out=fold_scale[:], in0=fold_sign[:], in1=radians[:], op=ALU.mult)

        COS, SIN = 0, 1
        trig = keep.tile([P, 2, PACK, PAIRS], F32)
        cos_t = trig[:, COS]
        sin_t = trig[:, SIN]

        def direct_tables(first, pairs):
            cols = slice(first, first + pairs)
            for t in range(PACK):
                nc.scalar.activation(out=sin_t[:, t, cols], in_=turns[:, cols], func=ACT.Sin, scale=token_radians[:, t : t + 1])
                nc.scalar.activation(out=cos_t[:, t, cols], in_=turns[:, cols], func=ACT.Sin, scale=token_radians_neg[:, t : t + 1], bias=math.pi / 2.0)

        def folded_tables(first):
            cols = slice(first, first + M_TILE)
            low = slice(first, first + COS_FOLD_PAIRS)
            high = slice(first + COS_FOLD_PAIRS, first + M_TILE)
            for t in range(PACK):
                nc.scalar.activation(out=sin_t[:, t, cols], in_=turns[:, cols], func=ACT.Sin, scale=fold_scale[:, 0, t : t + 1], bias=fold_bias[:, 0, t : t + 1])
                nc.scalar.activation(out=cos_t[:, t, low], in_=turns[:, low], func=ACT.Sin, scale=fold_scale[:, 1, t : t + 1], bias=fold_bias[:, 1, t : t + 1])
                nc.scalar.activation(out=cos_t[:, t, high], in_=turns[:, high], func=ACT.Sin, scale=token_radians_neg[:, t : t + 1], bias=math.pi / 2.0)

        wrapped = {}

        def wrap_a(u):
            cols = slice(UNITS[u], UNITS[u] + M_TILE)
            whole = angles.tile([P, PACK, M_TILE], I32, tag="whole")
            frac = angles.tile([P, PACK, M_TILE], F32, tag="frac")
            for t in range(PACK):
                nc.vector.tensor_scalar(out=whole[:, t, :], in0=turns[:, cols], scalar1=token[:, t : t + 1], scalar2=None, op0=ALU.mult)
            for t in range(PACK):
                nc.vector.scalar_tensor_tensor(out=frac[:, t, :], in0=turns[:, cols], scalar=token[:, t : t + 1], in1=whole[:, t, :], op0=ALU.mult, op1=ALU.subtract)
            wrapped[u] = frac

        def wrap_b(u):
            frac = wrapped[u]
            minus_q = angles.tile([P, PACK, M_TILE], F32, tag="minus_q")
            nc.vector.scalar_tensor_tensor(out=minus_q[:], in0=frac[:], scalar=0.25, in1=frac[:], op0=ALU.is_gt, op1=ALU.subtract)
            wrapped[u] = (frac, minus_q)

        def tables(u):
            first = UNITS[u]
            cols = slice(first, first + M_TILE)
            if first < WRAPPED_PAIRS:
                frac, minus_q = wrapped[u]
                nc.scalar.activation(out=sin_t[:, :, cols], in_=frac[:], func=ACT.Sin, scale=TWO_PI)
                nc.scalar.activation(out=cos_t[:, :, cols], in_=minus_q[:], func=ACT.Sin, scale=-TWO_PI, bias=math.pi / 2.0)
            elif first < FOLDED_PAIRS:
                folded_tables(first)
            else:
                direct_tables(first, M_TILE)

        x_codes = keep.tile([P, WIDTH], U32, align_bytes=64)
        x_scales = keep.tile([P, WIDTH], U8, align_bytes=64)
        x_grouped = [keep.tile([P, LOAD_COLS, PACK], BF16, name="x_grouped%d" % c, align_bytes=64) for c in range(LOADS)]

        def x_regroup(c):
            regroup(nc.scalar.copy if c in S_REGROUPS else nc.vector.tensor_copy, x_grouped[c][:], x_raw[c][:])

        def x_regroup_pe(c, half):
            half_cols = LOAD_COLS // 2
            bank = staging.tile([P, half_cols, PACK], BF16, name="staged")
            for q in (0, 1):
                cols = slice(half * half_cols + q * M_TILE, half * half_cols + (q + 1) * M_TILE)
                nc.tensor.matmul(
                    bank[:, q * M_TILE : (q + 1) * M_TILE, :].rearrange("p (c i) t -> p c t i", i=RUN), lhsT=identity[:],
                    rhs=x_raw[c][:, :, cols].rearrange("p t (c i) -> p c t i", i=RUN), start=True, stop=True,
                )
            return bank

        def x_collect(c, half, bank):
            half_cols = LOAD_COLS // 2
            nc.scalar.copy(out=x_grouped[c][:, half * half_cols : (half + 1) * half_cols, :], in_=bank[:])

        def x_quantise(c):
            cols = slice(c * LOAD_COLS, (c + 1) * LOAD_COLS)
            nc.vector.quantize_mx(out=x_codes[:, cols].bitcast(E4M3_X4), scales=x_scales[:, cols], in_=x_grouped[c][:].rearrange("p c t -> p (c t)"))

        gy_codes = keep.tile([P, 2, PAIRS], U32, align_bytes=64)
        gy_scales = keep.tile([P, 2, PAIRS], U8, align_bytes=64)

        full = {}
        result_tiles = {}

        def pass_(u, e, n):
            rows = slice(UNITS[u], UNITS[u] + M_TILE)
            cols = slice(n * N_TILE, (n + 1) * N_TILE)
            bank = banks.tile([P, N_TILE], F32, name="bank")
            nc.tensor.matmul_mx(
                out=bank[:], lhsT=gy_codes[:, e, rows].bitcast(E5M2_X4), lhsT_scale=gy_scales[:, e, rows],
                rhs=x_codes[:, cols].bitcast(E4M3_X4), rhs_scale=x_scales[:, cols], start=True, stop=True,
            )
            full[(u, e, n)] = bank

        def empty(u, e, n, copy):
            if (u, e) not in result_tiles:
                result_tiles[(u, e)] = results.tile([P, WIDTH], F32, name="result")
            copy(out=result_tiles[(u, e)][:, n * N_TILE : (n + 1) * N_TILE], in_=full[(u, e, n)][:])

        def store(u, e, n0, n1):
            cols = slice(n0 * N_TILE, n1 * N_TILE)
            nc.sync.dma_start(out=out_by_parity[e, UNITS[u] : UNITS[u] + M_TILE, cols], in_=result_tiles[(u, e)][:, cols])

        def multiply(u, e):
            for n in range(N_TILES):
                pass_(u, e, n)
            for n in range(N_TILES):
                if n not in V_BANKS.get((u, e), ()):
                    empty(u, e, n, nc.scalar.copy)

        def finish(u, e):
            for n in V_BANKS.get((u, e), ()):
                empty(u, e, n, nc.vector.tensor_copy)
            step = STORE_STEP.get((u, e), 2)
            for n in range(0, N_TILES, step):
                store(u, e, n, n + step)

        terms = {}
        grouped = {}
        g_pairs = {}

        def loaded(u):
            start = max(f for f, n in G_LOADS if f <= UNITS[u])
            return g_raw[start][:, :, 2 * (UNITS[u] - start) : 2 * (UNITS[u] - start + M_TILE)]

        def stage(u):
            bank = staging.tile([P, PACK, 2 * M_TILE], BF16, name="staged")
            for half in (slice(0, PACK // 2), slice(PACK // 2, PACK)):
                nc.tensor.matmul(bank[:, half, :], lhsT=identity[:], rhs=loaded(u)[:, half, :], start=True, stop=True)
            g_pairs[u] = bank[:].rearrange("p t (i e) -> p e t i", e=2)

        def products(u, e):
            if u not in g_pairs:
                g_pairs[u] = loaded(u).rearrange("p t (i e) -> p e t i", e=2)
            term = work.tile([P, 2, PACK, M_TILE], F32, tag="term%d" % e)
            factors = trig[:, :, :, UNITS[u] : UNITS[u] + M_TILE]
            if e == 0:
                nc.vector.tensor_tensor(out=term[:], in0=g_pairs[u], in1=factors, op=ALU.mult)
            else:
                for k in (0, 1):
                    nc.vector.tensor_tensor(out=term[:, k], in0=g_pairs[u][:, k], in1=factors[:, 1 - k], op=ALU.mult)
            terms[(u, e)] = term

        def combine(u, e):
            on_g = (u, e) in G_SUMS
            pool = sums if on_g else work
            tile = pool.tile([P, M_TILE, PACK], BF16, align_bytes=64, name="summed" if on_g else "grouped%d" % e)
            runs = terms[(u, e)][:].rearrange("p k t (c i) -> p k c t i", i=4)
            (nc.gpsimd if on_g else nc.vector).tensor_tensor(
                out=tile[:].rearrange("p (c i) t -> p c t i", i=4),
                in0=runs[:, e], in1=runs[:, 1 - e],
                op=(ALU.add if e == 0 else ALU.subtract),
            )
            grouped[(u, e)] = tile

        def quantise(u, e):
            cols = slice(UNITS[u], UNITS[u] + M_TILE)
            nc.vector.quantize_mx(out=gy_codes[:, e, cols].bitcast(E5M2_X4), scales=gy_scales[:, e, cols], in_=grouped[(u, e)][:].rearrange("p c t -> p (c t)"))

        def first_banks(n):
            for e in (0, 1):
                pass_(0, e, n)
                empty(0, e, n, nc.scalar.copy)
                store(0, e, n, n + 1)

        tables(0)
        tables(1)
        wrap_a(FW)
        x_regroup(0)
        products(0, 0)
        wrap_b(FW)
        combine(0, 0)
        products(0, 1)
        quantise(0, 0)
        x_first = x_regroup_pe(1, 0)
        x_second = x_regroup_pe(1, 1)
        x_collect(1, 0, x_first)
        combine(0, 1)
        x_quantise(0)
        pass_(0, 0, 0)
        quantise(0, 1)
        pass_(0, 1, 0)
        x_regroup(2)
        x_collect(1, 1, x_second)
        tables(2)
        empty(0, 0, 0, nc.scalar.copy)
        store(0, 0, 0, 1)
        empty(0, 1, 0, nc.scalar.copy)
        store(0, 1, 0, 1)
        x_quantise(1)
        x_regroup(3)
        x_quantise(2)
        first_banks(1)
        stage(1)
        first_banks(2)
        stage(2)
        tables(3)
        x_quantise(3)
        first_banks(3)
        for k in range(LATE_LOADS, len(G_LOADS)):
            load_g(k)
        tables(FW)

        unquantised = None
        unfinished = []

        def close(half):
            quantise(*half)
            multiply(*half)
            unfinished.append(half)

        def finish_all(count):
            for half in unfinished[:count]:
                finish(*half)
            for half in list(unfinished[:count]):
                unfinished.remove(half)

        for u in range(1, len(UNITS)):
            if u + 1 in STAGED and u >= 2:
                stage(u + 1)
            if u in MIXED:
                products(u, 0)
                if unquantised:
                    close(unquantised)
                    unquantised = None
                combine(u, 0)
                products(u, 1)
                finish_all(len(unfinished))
                for e in (0, 1):
                    for j in WRAP_A.get((u, e), ()):
                        wrap_a(j)
                    for j in WRAP_B.get((u, e), ()):
                        wrap_b(j)
                combine(u, 1)
                quantise(u, 0)
                for e in (0, 1):
                    for j in TABLES.get((u, e), ()):
                        tables(j)
                multiply(u, 0)
                quantise(u, 1)
                multiply(u, 1)
                for e in (0, 1):
                    for j in TABLES_LATER.get((u, e), ()):
                        tables(j)
                unfinished.extend([(u, 0), (u, 1)])
            else:
                for e in (0, 1):
                    products(u, e)
                    finish_all(len(unfinished))
                    for j in WRAP_A.get((u, e), ()):
                        wrap_a(j)
                    for j in WRAP_B.get((u, e), ()):
                        wrap_b(j)
                    if unquantised:
                        quantise(*unquantised)
                    for j in TABLES.get((u, e), ()):
                        tables(j)
                    if unquantised:
                        multiply(*unquantised)
                        unfinished.append(unquantised)
                    for j in TABLES_LATER.get((u, e), ()):
                        tables(j)
                    combine(u, e)
                    unquantised = (u, e)
        if unquantised:
            close(unquantised)
        finish_all(len(unfinished))
